import numpy as np
import ml_dtypes


def mxq(x, axis, fmt="e4m3"):
    dtype, down = {"e4m3": (ml_dtypes.float8_e4m3fn, 7), "e5m2": (ml_dtypes.float8_e5m2, 14)}[fmt]
    v = np.moveaxis(np.asarray(x, np.float32).astype(ml_dtypes.bfloat16).astype(np.float64), axis, -1)
    blocks = v.reshape(v.shape[:-1] + (-1, 32))
    amax = np.abs(blocks).max(-1, keepdims=True)
    byte = np.maximum(np.where(amax > 0, np.frexp(amax)[1] - 1 + 127, 0) - down, 1)
    scale = np.exp2(byte - 127.0)
    codes = (blocks / scale).astype(np.float32).astype(dtype).astype(np.float64)
    return np.moveaxis((codes * scale).reshape(v.shape), -1, axis)


WIDE = False


def mx_kscale(k):
    if not WIDE:
        return np.ones(k)
    levels = np.array([10, -10, 5, -5, 0])
    if k % 512:
        return np.exp2(np.random.permutation(np.resize(levels, k // 32))).repeat(32)
    a = np.empty((k // 512, 16))
    for p in range(k // 512):
        a[p, :8] = np.random.permutation(np.resize(levels, 8))
        for g in range(8):
            far = levels[np.abs(levels - a[p, g]) >= 10]
            a[p, g + 8] = far[np.random.randint(len(far))]
    return np.exp2(a.ravel()).repeat(32)


BF16 = ml_dtypes.bfloat16


def bf(x):
    return np.asarray(x, np.float32).astype(BF16)


def f64(x):
    return np.asarray(x).astype(np.float64)


B, In, H, Hh, E, G = 512, 1024, 1024, 256, 128, 4
EPS = 1e-6


def rn(*shape):
    return np.random.standard_normal(shape)


def sigmoid(v):
    return 1.0 / (1.0 + np.exp(-v))


def ln(a, gamma, beta):
    mean = a.mean(-1, keepdims=True)
    std = a.std(-1, keepdims=True, ddof=1)
    return gamma * (a - mean) / (std + EPS) + beta


def expand(emb, w):
    return (emb.transpose(1, 0, 2) @ w.transpose(0, 2, 1)).transpose(1, 0, 2)


def setup_inputs():
    s, t = mx_kscale(In), mx_kscale(H)
    return {
        'x': bf(rn(B, In) * s),
        'h': bf(rn(B, H) * t),
        'c': bf(rn(B, H)),
        'emb_h': bf(1.0 + 0.5 * rn(B, G, E)),
        'emb_x': bf(1.0 + 0.5 * rn(B, G, E)),
        'emb_b': bf(rn(B, G, E)),
        'Wsh': bf(1.0 / E + 0.5 * rn(G, H, E) / np.sqrt(E)),
        'Wsx': bf(1.0 / E + 0.5 * rn(G, H, E) / np.sqrt(E)),
        'Wsb': bf(0.5 * rn(G, H, E) / np.sqrt(E)),
        'Wih': bf(rn(G * H, In) / np.sqrt(In) / s[None, :]),
        'Whh': bf(rn(G * H, H) / np.sqrt(H) / t[None, :]),
        'bias': bf(0.3 * rn(G * H)),
        'ln_gamma': bf(1.0 + 0.1 * rn(G, H)),
        'ln_beta': bf(0.1 * rn(G, H)),
        'lnc_gamma': bf(1.0 + 0.1 * rn(H)),
        'lnc_beta': bf(0.1 * rn(H)),
    }


def reference(x, h, c, emb_h, emb_x, emb_b, Wsh, Wsx, Wsb, Wih, Whh, bias, ln_gamma, ln_beta, lnc_gamma, lnc_beta):
    zh = expand(f64(emb_h), f64(Wsh))
    zx = expand(f64(emb_x), f64(Wsx))
    zb = expand(f64(emb_b), f64(Wsb))
    xh = (mxq(f64(x), 1, 'e4m3') @ mxq(f64(Wih).T, 0, 'e4m3')).reshape(B, G, H)
    hh = (mxq(f64(h), 1, 'e4m3') @ mxq(f64(Whh).T, 0, 'e4m3')).reshape(B, G, H)
    gates = xh * zx + hh * zh + (f64(bias).reshape(G, H) + zb)
    gates = ln(gates, f64(ln_gamma), f64(ln_beta))
    i, f, g, o = gates[:, 0], gates[:, 1], gates[:, 2], gates[:, 3]
    new_c = f64(c) * sigmoid(f) + sigmoid(i) * np.tanh(g)
    new_c = ln(new_c, f64(lnc_gamma), f64(lnc_beta))
    new_h = np.tanh(new_c) * sigmoid(o)
    return new_h, new_c

@@ -1,0 +1,436 @@
+import math
+from contextlib import ExitStack
+
+import concourse.mybir as mybir
+from concourse.masks import make_identity
+
+F32 = mybir.dt.float32
+BF16 = mybir.dt.bfloat16
+U32 = mybir.dt.uint32
+U8 = mybir.dt.uint8
+FP8X4 = mybir.dt.float8_e4m3fn_x4
+ACT = mybir.ActivationFunctionType
+ALU = mybir.AluOpType
+
+P = 128
+B = 512
+K = 1024
+H = 1024
+E = 128
+GATES = 4
+BATCH_TILES = B // P
+K_PASS = 4 * P
+PASSES = K // K_PASS
+ROWS = 512
+HALVES = H // ROWS
+TILES_PER_GATE = HALVES * BATCH_TILES
+N_TILES = GATES * TILES_PER_GATE
+EPS = 1e-6
+
+GATE_I, GATE_F, GATE_G, GATE_O = 0, 1, 2, 3
+GATE_ORDER = (GATE_I, GATE_G, GATE_F, GATE_O)
+FIRST_BIAS_ROW_GATE = 1
+
+STEPS_PER_HALF_GATE = 2 * PASSES
+N_STEPS = GATES * HALVES * STEPS_PER_HALF_GATE
+QUANTISE_AHEAD = STEPS_PER_HALF_GATE + 1
+TURN_AHEAD = QUANTISE_AHEAD + 1
+LOAD_AHEAD = 4
+LAST_LAG = 2
+UNIT_BLOCKS = H // P
+VECTOR_HELPS_UNTIL = 2 * TILES_PER_GATE
+BLOCKS_PER_SLOT = 2
+FIRST_BACK_SLOT = 1 + UNIT_BLOCKS // BLOCKS_PER_SLOT
+BACK_PER_SLOT = 2
+
+FLOPS = 2 * (2 * B * K * GATES * H) + 3 * (2 * B * E * GATES * H)
+
+
+def where(t):
+    return t // TILES_PER_GATE, (t % TILES_PER_GATE) // BATCH_TILES, t % BATCH_TILES
+
+
+def completed_row(t):
+    if 0 <= t < N_TILES and where(t)[1] == HALVES - 1:
+        return where(t)[0], where(t)[2]
+    return None
+
+
+def tile_hyperlstmcell_pb_kernel(
+    tc, x, h, c, emb_h, emb_x, emb_b, Wsh, Wsx, Wsb, Wih, Whh, bias,
+    ln_gamma, ln_beta, lnc_gamma, lnc_beta, out_0, out_1,
+):
+    nc = tc.nc
+    big_weight = {"x": Wih, "h": Whh}
+    small_weight = {"x": Wsx, "h": Wsh, "b": Wsb}
+    embedding = {"x": emb_x, "h": emb_h, "b": emb_b}
+
+    with ExitStack() as ctx:
+        const = ctx.enter_context(tc.tile_pool(name="const", bufs=1))
+        keep = ctx.enter_context(tc.tile_pool(name="keep", bufs=1))
+        big_rows = ctx.enter_context(tc.tile_pool(name="big_rows", bufs=3))
+        small_rows = ctx.enter_context(tc.tile_pool(name="small_rows", bufs=3))
+        grouped_pool = ctx.enter_context(tc.tile_pool(name="grouped", bufs=3))
+        half_gate = ctx.enter_context(tc.tile_pool(name="half_gate", bufs=2))
+        per_gate = ctx.enter_context(tc.tile_pool(name="per_gate", bufs=2))
+        work = ctx.enter_context(tc.tile_pool(name="work", bufs=2))
+        z_pool = ctx.enter_context(tc.tile_pool(name="z_sb", bufs=2))
+        pre_pool = ctx.enter_context(tc.tile_pool(name="pre", bufs=8))
+        sums_pool = ctx.enter_context(tc.tile_pool(name="sums", bufs=6))
+        scaled_pool = ctx.enter_context(tc.tile_pool(name="scaled", bufs=2))
+        block_pool = ctx.enter_context(tc.tile_pool(name="block", bufs=3))
+        cell_rows = ctx.enter_context(tc.tile_pool(name="cell_rows", bufs=BATCH_TILES))
+        scratch = ctx.enter_context(tc.tile_pool(name="scratch", bufs=2))
+        results = ctx.enter_context(tc.tile_pool(name="results", bufs=2))
+        stats = ctx.enter_context(tc.tile_pool(name="stats", bufs=4))
+        psum_out = ctx.enter_context(tc.psum_pool(name="psum_out", bufs=1))
+        psum_turn = ctx.enter_context(tc.psum_pool(name="psum_turn", bufs=3))
+
+        ident_f32 = const.tile([P, P], F32)
+        make_identity(nc, ident_f32[:])
+        ident_bf16 = const.tile([P, P], BF16)
+        make_identity(nc, ident_bf16[:])
+        exp_half = const.tile([P, 1], F32)
+        nc.vector.memset(exp_half[:], 0.5)
+        exp_minus_one = const.tile([P, 1], F32)
+        nc.vector.memset(exp_minus_one[:], -1.0)
+
+        def load_rows(dram_rows):
+            rows_sb = big_rows.tile([P, ROWS // P, K], BF16)
+            nc.sync.dma_start(out=rows_sb[:], in_=dram_rows.rearrange("(r p) k -> p r k", p=P))
+            return rows_sb
+
+        def turn(rows_sb, g, vector_helps):
+            grouped = grouped_pool.tile([P, 4 * ROWS], BF16, align_bytes=64)
+            grouped_words = grouped[:].bitcast(F32).rearrange("p (r u) -> p r u", u=2)
+            for pair in range(2):
+                bank = psum_turn.tile([P, 2, 2 * P], F32, tag="turned")
+                for u in range(2):
+                    for r in range(2):
+                        words = slice(2 * P * g + u, 2 * P * (g + 1), 2)
+                        nc.tensor.transpose(
+                            bank[:, u, r * P : (r + 1) * P],
+                            rows_sb[:, 2 * pair + r, :].bitcast(F32)[:, words],
+                            ident_f32[:],
+                        )
+                target = grouped_words[:, 2 * P * pair : 2 * P * (pair + 1), :]
+                if vector_helps and pair == 1:
+                    nc.vector.tensor_copy(out=target, in_=bank[:].rearrange("p u r -> p r u"))
+                else:
+                    nc.scalar.copy(out=target, in_=bank[:].rearrange("p u r -> p r u"))
+            return grouped
+
+        def quantise(grouped, codes, scales):
+            nc.vector.quantize_mx(out=codes.bitcast(FP8X4), scales=scales, in_=grouped[:])
+
+        def transpose_eight(blocks, dst):
+            bank = psum_turn.tile([P, 8 * P], BF16, tag="turned")
+            for i, block in enumerate(blocks):
+                nc.tensor.transpose(bank[:, i * P : (i + 1) * P], block, ident_bf16[:])
+            nc.scalar.copy(out=dst, in_=bank[:])
+
+        def load_small_weights(position, parts):
+            gate = GATE_ORDER[position]
+            for name in ("x", "h", "b"):
+                parts["rows_" + name] = small_rows.tile([P, H // P, E], BF16, name="rows_" + name, tag="rows")
+                nc.sync.dma_start(
+                    out=parts["rows_" + name][:], in_=small_weight[name][gate].rearrange("(j p) e -> p j e", p=P)
+                )
+
+        def turn_small_weight(name, parts):
+            parts["small_" + name] = per_gate.tile([P, H], BF16, name="small_" + name)
+            transpose_eight([parts["rows_" + name][:, j, :] for j in range(H // P)], parts["small_" + name][:])
+
+        def start_tile(t):
+            position, half, m = where(t)
+            gate = GATE_ORDER[position]
+            samples = slice(m * P, (m + 1) * P)
+            units = slice(half * ROWS, (half + 1) * ROWS)
+            parts = gate_parts[position]
+            weights = half_gate_weights[t // BATCH_TILES]
+            tile = {}
+            for name in ("x", "h"):
+                tile["z_" + name] = psum_out.tile([P, ROWS], F32, name="z_" + name)
+                nc.tensor.matmul(
+                    out=tile["z_" + name][:], lhsT=emb_t[name][:, gate, samples], rhs=parts["small_" + name][:, units],
+                    start=True, stop=True,
+                )
+            for name in ("x", "h"):
+                tile["z_sb_" + name] = z_pool.tile([P, ROWS], F32, name="z_sb_" + name)
+                nc.scalar.copy(out=tile["z_sb_" + name][:], in_=tile["z_" + name][:])
+                tile["product_" + name] = psum_out.tile([P, ROWS], F32, name="product_" + name)
+                for g in range(PASSES):
+                    nc.tensor.matmul_mx(
+                        out=tile["product_" + name][:],
+                        lhsT=act_codes[name][:, g, samples].bitcast(FP8X4),
+                        lhsT_scale=act_scales[name][:, g, samples],
+                        rhs=weights["codes_" + name][:, g, :].bitcast(FP8X4),
+                        rhs_scale=weights["scales_" + name][:, g, :],
+                        start=(g == 0),
+                        stop=(g == PASSES - 1),
+                    )
+            return tile
+
+        def start_offset(t, tile):
+            position, half, m = where(t)
+            gate = GATE_ORDER[position]
+            units = slice(half * ROWS, (half + 1) * ROWS)
+            tile["z_b"] = psum_out.tile([P, ROWS], F32, name="z_b")
+            nc.tensor.matmul(
+                out=tile["z_b"][:], lhsT=emb_t["b"][:, gate, m * P : (m + 1) * P], rhs=gate_parts[position]["small_b"][:, units],
+                start=True, stop=(position == 0),
+            )
+            if position > 0:
+                first_unit = (gate - FIRST_BIAS_ROW_GATE) * H + half * ROWS
+                nc.tensor.matmul(
+                    out=tile["z_b"][:], lhsT=ones[:], rhs=bias_rows[:, first_unit : first_unit + ROWS], start=False, stop=True,
+                )
+
+        def read_psum(t, tile):
+            for name in ("x", "h"):
+                tile["term_" + name] = work.tile([P, ROWS], F32, name="term_" + name)
+                nc.vector.tensor_tensor(
+                    out=tile["term_" + name][:], in0=tile["product_" + name][:], in1=tile["z_sb_" + name][:], op=ALU.mult,
+                )
+
+        def add_products(tile):
+            nc.vector.tensor_tensor(out=tile["term_x"][:], in0=tile["term_x"][:], in1=tile["term_h"][:], op=ALU.add)
+
+        def finish_tile(t, tile):
+            position, half, m = where(t)
+            units = slice(half * ROWS, (half + 1) * ROWS)
+            if half == 0:
+                rows[position, m] = {
+                    "pre": pre_pool.tile([P, H], F32, name="pre"),
+                    "sums": sums_pool.tile([P, HALVES], F32, name="sums"),
+                }
+            row = rows[position, m]
+            if position == 0:
+                nc.vector.tensor_tensor(out=tile["term_x"][:], in0=tile["term_x"][:], in1=first_bias[:, units], op=ALU.add)
+            nc.vector.scalar_tensor_tensor(
+                out=row["pre"][:, units], in0=tile["z_b"][:], scalar=1.0, in1=tile["term_x"][:],
+                op0=ALU.mult, op1=ALU.add, accum_out=row["sums"][:, half : half + 1],
+            )
+
+        def start_stats(values, sums):
+            neg_mean = stats.tile([P, 1], F32)
+            nc.gpsimd.tensor_scalar(
+                out=neg_mean[:], in0=sums[:, 0:1], scalar1=sums[:, 1:2], scalar2=-1.0 / H, op0=ALU.add, op1=ALU.mult,
+            )
+            squares = scratch.tile([P, H], BF16)
+            sum_sq = stats.tile([P, 1], F32)
+            nc.scalar.activation(
+                out=squares[:], in_=values, func=ACT.Square, bias=neg_mean[:, 0:1], scale=1.0, accum_out=sum_sq[:],
+            )
+            root = stats.tile([P, 1], F32)
+            nc.gpsimd.tensor_tensor(out=root[:], in0=sum_sq[:], in1=exp_half[:], op=ALU.pow)
+            std_eps = stats.tile([P, 1], F32)
+            nc.gpsimd.tensor_scalar(
+                out=std_eps[:], in0=root[:], scalar1=1.0 / math.sqrt(H - 1), scalar2=EPS, op0=ALU.mult, op1=ALU.add,
+            )
+            inv_std = stats.tile([P, 1], F32)
+            nc.gpsimd.tensor_tensor(out=inv_std[:], in0=std_eps[:], in1=exp_minus_one[:], op=ALU.pow)
+            return neg_mean, inv_std
+
+        def centre_and_gain(out, values, neg_mean, gain):
+            nc.vector.scalar_tensor_tensor(
+                out=out, in0=values, scalar=neg_mean[:, 0:1], in1=gain, op0=ALU.add, op1=ALU.mult,
+            )
+
+        def scale_and_shift(values, inv_std, shift):
+            nc.vector.scalar_tensor_tensor(
+                out=values, in0=values, scalar=inv_std[:, 0:1], in1=shift, op0=ALU.mult, op1=ALU.add,
+            )
+
+        def gate_block(position, j):
+            gate = GATE_ORDER[position]
+            block = slice(j * P, (j + 1) * P)
+            bank = psum_turn.tile([P, B], F32, tag="turned")
+            for m in range(BATCH_TILES):
+                nc.tensor.transpose(bank[:, m * P : (m + 1) * P], rows[position, m]["pre"][:, block], ident_f32[:])
+            column = gate * UNIT_BLOCKS + j
+            gain = unit_columns[:, column : column + 1]
+            shift = unit_columns[:, GATES * UNIT_BLOCKS + column : GATES * UNIT_BLOCKS + column + 1]
+            if gate == GATE_I:
+                nc.scalar.activation(out=cell_t[:, j, :], in_=bank[:], func=ACT.Sigmoid, scale=gain, bias=shift)
+                return
+            activated = block_pool.tile([P, B], F32)
+            if gate == GATE_G:
+                nc.scalar.activation(out=activated[:], in_=bank[:], func=ACT.Tanh, scale=gain, bias=shift)
+                nc.vector.tensor_tensor(out=cell_t[:, j, :], in0=cell_t[:, j, :], in1=activated[:], op=ALU.mult)
+            else:
+                nc.scalar.activation(out=activated[:], in_=bank[:], func=ACT.Sigmoid, scale=gain, bias=shift)
+                c_bank = psum_turn.tile([P, B], BF16, tag="turned")
+                for m in range(BATCH_TILES):
+                    nc.tensor.transpose(c_bank[:, m * P : (m + 1) * P], c_sb[:, m, block], ident_bf16[:])
+                nc.vector.tensor_tensor(out=activated[:], in0=c_bank[:], in1=activated[:], op=ALU.mult)
+                nc.vector.tensor_tensor(out=cell_t[:, j, :], in0=cell_t[:, j, :], in1=activated[:], op=ALU.add)
+
+        def cell_back(m):
+            row = {
+                "values": cell_rows.tile([P, H], F32, name="cell_row"),
+                "sums": sums_pool.tile([P, HALVES], F32, name="cell_sums"),
+            }
+            for half in range(HALVES):
+                bank = psum_turn.tile([P, ROWS], F32, tag="turned")
+                for i in range(ROWS // P):
+                    nc.tensor.transpose(
+                        bank[:, i * P : (i + 1) * P], cell_t[:, half * (ROWS // P) + i, m * P : (m + 1) * P], ident_f32[:],
+                    )
+                nc.scalar.activation(
+                    out=row["values"][:, half * ROWS : (half + 1) * ROWS], in_=bank[:], func=ACT.Identity,
+                    accum_out=row["sums"][:, half : half + 1],
+                )
+            row["neg_mean"], row["inv_std"] = start_stats(row["values"][:], row["sums"])
+            return row
+
+        def finish_cell(m, row):
+            new_c = results.tile([P, H], F32, tag="result")
+            centre_and_gain(new_c[:], row["values"][:], row["neg_mean"], free_axis_vectors["gain_c"][:])
+            scale_and_shift(new_c[:], row["inv_std"], free_axis_vectors["shift_c"][:])
+            nc.sync.dma_start(out=out_1[m * P : (m + 1) * P, :], in_=new_c[:])
+            nc.scalar.activation(out=row["values"][:], in_=new_c[:], func=ACT.Tanh)
+
+        gate_parts = {position: {} for position in range(GATES)}
+        first_bias = keep.tile([P, H], BF16)
+        nc.gpsimd.dma_start(out=first_bias[:], in_=bias[GATE_ORDER[0] * H : (GATE_ORDER[0] + 1) * H].partition_broadcast(P))
+        ones = const.tile([P, P], BF16)
+        nc.vector.memset(ones[:], 1.0)
+        bias_rows = keep.tile([P, (GATES - FIRST_BIAS_ROW_GATE) * H], BF16)
+        nc.vector.memset(bias_rows[:], 0.0)
+        nc.sync.dma_start(out=bias_rows[0:1, :], in_=bias[FIRST_BIAS_ROW_GATE * H :].unsqueeze(0))
+        act_rows = {"x": load_rows(x), "h": load_rows(h)}
+        emb_rows = {}
+        for name in ("x", "h", "b"):
+            emb_rows[name] = pre_pool.tile([P, BATCH_TILES, GATES * E], BF16, name="emb_rows_" + name, tag="pre")
+            nc.sync.dma_start(out=emb_rows[name][:], in_=embedding[name].rearrange("(m p) g e -> p m (g e)", p=P))
+        load_small_weights(0, gate_parts[0])
+        vector_rows = const.tile([P, P], BF16)
+        nc.vector.memset(vector_rows[:], 0.0)
+        for first_row, vector in ((0, ln_gamma), (GATES * UNIT_BLOCKS, ln_beta)):
+            nc.sync.dma_start(
+                out=vector_rows[first_row : first_row + GATES * UNIT_BLOCKS, :],
+                in_=vector.rearrange("g (j p) -> (g j) p", p=P),
+            )
+
+        act_codes, act_scales = {}, {}
+        for name in ("x", "h"):
+            act_codes[name] = keep.tile([P, PASSES, B], U32, align_bytes=64, name="act_codes_" + name)
+            act_scales[name] = keep.tile([P, PASSES, B], U8, align_bytes=64, name="act_scales_" + name)
+            for g in range(PASSES):
+                quantise(turn(act_rows[name], g, True), act_codes[name][:, g, :], act_scales[name][:, g, :])
+
+        emb_t = {}
+        for name in ("x", "h", "b"):
+            emb_t[name] = keep.tile([P, GATES, B], BF16, name="emb_t_" + name)
+            for first_gate in range(0, GATES, 2):
+                transpose_eight(
+                    [
+                        emb_rows[name][:, m, gate * E : (gate + 1) * E]
+                        for gate in (first_gate, first_gate + 1)
+                        for m in range(BATCH_TILES)
+                    ],
+                    emb_t[name][:, first_gate : first_gate + 2, :].rearrange("p g b -> p (g b)"),
+                )
+            turn_small_weight(name, gate_parts[0])
+
+        vector_bank = psum_turn.tile([P, P], BF16, tag="turned")
+        nc.tensor.transpose(vector_bank[:], vector_rows[:], ident_bf16[:])
+        unit_columns = const.tile([P, P], F32)
+        nc.scalar.copy(out=unit_columns[:], in_=vector_bank[:])
+
+        c_sb = keep.tile([P, BATCH_TILES, H], BF16)
+        cell_t = keep.tile([P, UNIT_BLOCKS, B], F32)
+        free_axis_vectors = {}
+
+        step_rows, step_grouped, half_gate_weights, tiles, rows, cell_state = {}, {}, {}, {}, {}, {}
+        for t in range(-(TURN_AHEAD + LOAD_AHEAD), N_TILES + LAST_LAG):
+            has_tile = 0 <= t < N_TILES
+            row0, row1, row2 = [completed_row(t - lag) for lag in range(LAST_LAG + 1)]
+
+            if has_tile:
+                read_psum(t, tiles[t])
+            if row1 is not None and GATE_ORDER[row1[0]] == GATE_O:
+                row = rows[row1]
+                row["scaled"] = scaled_pool.tile([P, H], F32, name="scaled")
+                centre_and_gain(row["scaled"][:], row["pre"][:], row["neg_mean"], free_axis_vectors["gain_o"][:])
+            if 0 <= t + 1 < N_TILES:
+                tiles[t + 1] = start_tile(t + 1)
+
+            q = t + TURN_AHEAD + LOAD_AHEAD
+            if 0 <= q < N_STEPS and q % PASSES == 0:
+                first_row = GATE_ORDER[q // (HALVES * STEPS_PER_HALF_GATE)] * H + (q // STEPS_PER_HALF_GATE) % HALVES * ROWS
+                matrix = big_weight[("x", "h")[(q % STEPS_PER_HALF_GATE) // PASSES]]
+                step_rows[q // PASSES] = load_rows(matrix[first_row : first_row + ROWS, :])
+            q = t + TURN_AHEAD
+            if 0 <= q < N_STEPS:
+                step_grouped[q] = turn(step_rows[q // PASSES], q % PASSES, t < VECTOR_HELPS_UNTIL)
+
+            if has_tile and t // TILES_PER_GATE + 1 < GATES:
+                next_position, slot_in_gate = t // TILES_PER_GATE + 1, t % TILES_PER_GATE
+                if slot_in_gate == 0:
+                    load_small_weights(next_position, gate_parts[next_position])
+                if slot_in_gate in (1, 2, 3):
+                    turn_small_weight(("x", "h", "b")[slot_in_gate - 1], gate_parts[next_position])
+            if t == 0:
+                nc.sync.dma_start(out=c_sb[:], in_=c.rearrange("(m p) n -> p m n", p=P))
+                for name, vector in (
+                    ("gain_c", lnc_gamma), ("shift_c", lnc_beta),
+                    ("gain_o", ln_gamma[GATE_O, :]), ("shift_o", ln_beta[GATE_O, :]),
+                ):
+                    free_axis_vectors[name] = keep.tile([P, H], BF16, name=name)
+                    nc.gpsimd.dma_start(out=free_axis_vectors[name][:], in_=vector.partition_broadcast(P))
+
+            if has_tile:
+                add_products(tiles[t])
+            q = t + QUANTISE_AHEAD
+            if 0 <= q < N_STEPS:
+                if q % STEPS_PER_HALF_GATE == 0:
+                    weights = {}
+                    for name in ("x", "h"):
+                        weights["codes_" + name] = half_gate.tile([P, PASSES, ROWS], U32, align_bytes=64, name="codes_" + name)
+                        weights["scales_" + name] = half_gate.tile([P, PASSES, ROWS], U8, align_bytes=64, name="scales_" + name)
+                    half_gate_weights[q // STEPS_PER_HALF_GATE] = weights
+                weights = half_gate_weights[q // STEPS_PER_HALF_GATE]
+                name, g = ("x", "h")[(q % STEPS_PER_HALF_GATE) // PASSES], q % PASSES
+                quantise(step_grouped[q], weights["codes_" + name][:, g, :], weights["scales_" + name][:, g, :])
+            if has_tile:
+                finish_tile(t, tiles[t])
+            if 0 <= t + 1 < N_TILES:
+                start_offset(t + 1, tiles[t + 1])
+
+            if row0 is not None:
+                row = rows[row0]
+                row["neg_mean"], row["inv_std"] = start_stats(row["pre"][:], row["sums"])
+            if row1 is not None:
+                row = rows[row1]
+                if GATE_ORDER[row1[0]] == GATE_O:
+                    scale_and_shift(row["scaled"][:], row["inv_std"], free_axis_vectors["shift_o"][:])
+                    nc.scalar.activation(out=row["scaled"][:], in_=row["scaled"][:], func=ACT.Sigmoid)
+                else:
+                    offset = stats.tile([P, 1], F32)
+                    nc.gpsimd.tensor_tensor(out=offset[:], in0=row["neg_mean"][:], in1=row["inv_std"][:], op=ALU.mult)
+                    nc.scalar.activation(
+                        out=row["pre"][:], in_=row["pre"][:], func=ACT.Identity, scale=row["inv_std"][:, 0:1], bias=offset[:, 0:1],
+                    )
+
+            if has_tile and t >= TILES_PER_GATE:
+                previous, slot_in_gate = t // TILES_PER_GATE - 1, t % TILES_PER_GATE
+                if 1 <= slot_in_gate < FIRST_BACK_SLOT:
+                    for j in range((slot_in_gate - 1) * BLOCKS_PER_SLOT, slot_in_gate * BLOCKS_PER_SLOT):
+                        gate_block(previous, j)
+                if GATE_ORDER[previous] == GATE_F:
+                    first = (slot_in_gate - FIRST_BACK_SLOT - 1) * BACK_PER_SLOT
+                    if 0 <= first < BATCH_TILES:
+                        for m in range(first, first + BACK_PER_SLOT):
+                            finish_cell(m, cell_state[m])
+                    first = (slot_in_gate - FIRST_BACK_SLOT) * BACK_PER_SLOT
+                    if 0 <= first < BATCH_TILES:
+                        for m in range(first, first + BACK_PER_SLOT):
+                            cell_state[m] = cell_back(m)
+
+            if row2 is not None and GATE_ORDER[row2[0]] == GATE_O:
+                m = row2[1]
+                new_h = results.tile([P, H], F32, tag="result")
+                nc.vector.tensor_tensor(out=new_h[:], in0=rows[row2]["scaled"][:], in1=cell_state[m]["values"][:], op=ALU.mult)
+                nc.sync.dma_start(out=out_0[m * P : (m + 1) * P, :], in_=new_h[:])

@@ -38,7 +38,7 @@ TURN_AHEAD = QUANTISE_AHEAD + 1
 LOAD_AHEAD = 4
 LAST_LAG = 2
 UNIT_BLOCKS = H // P
-VECTOR_HELPS_UNTIL = 2 * TILES_PER_GATE
+VECTOR_HELPS_UNTIL = 0
 BLOCKS_PER_SLOT = 2
 FIRST_BACK_SLOT = 1 + UNIT_BLOCKS // BLOCKS_PER_SLOT
 BACK_PER_SLOT = 2

@@ -77,7 +77,6 @@ def tile_hyperlstmcell_pb_kernel(
         z_pool = ctx.enter_context(tc.tile_pool(name="z_sb", bufs=2))
         pre_pool = ctx.enter_context(tc.tile_pool(name="pre", bufs=8))
         sums_pool = ctx.enter_context(tc.tile_pool(name="sums", bufs=6))
-        scaled_pool = ctx.enter_context(tc.tile_pool(name="scaled", bufs=2))
         block_pool = ctx.enter_context(tc.tile_pool(name="block", bufs=3))
         cell_rows = ctx.enter_context(tc.tile_pool(name="cell_rows", bufs=BATCH_TILES))
         scratch = ctx.enter_context(tc.tile_pool(name="scratch", bufs=2))
@@ -129,13 +128,12 @@ def tile_hyperlstmcell_pb_kernel(
                 nc.tensor.transpose(bank[:, i * P : (i + 1) * P], block, ident_bf16[:])
             nc.scalar.copy(out=dst, in_=bank[:])
 
-        def load_small_weights(position, parts):
+        def load_small_weight(position, name, parts):
             gate = GATE_ORDER[position]
-            for name in ("x", "h", "b"):
-                parts["rows_" + name] = small_rows.tile([P, H // P, E], BF16, name="rows_" + name, tag="rows")
-                nc.sync.dma_start(
-                    out=parts["rows_" + name][:], in_=small_weight[name][gate].rearrange("(j p) e -> p j e", p=P)
-                )
+            parts["rows_" + name] = small_rows.tile([P, H // P, E], BF16, name="rows_" + name, tag="rows")
+            nc.sync.dma_start(
+                out=parts["rows_" + name][:], in_=small_weight[name][gate].rearrange("(j p) e -> p j e", p=P)
+            )
 
         def turn_small_weight(name, parts):
             parts["small_" + name] = per_gate.tile([P, H], BF16, name="small_" + name)
@@ -252,19 +250,18 @@ def tile_hyperlstmcell_pb_kernel(
             gain = unit_columns[:, column : column + 1]
             shift = unit_columns[:, GATES * UNIT_BLOCKS + column : GATES * UNIT_BLOCKS + column + 1]
             if gate == GATE_I:
-                nc.scalar.activation(out=cell_t[:, j, :], in_=bank[:], func=ACT.Sigmoid, scale=gain, bias=shift)
+                nc.scalar.activation(out=cell_i[:, j, :], in_=bank[:], func=ACT.Sigmoid, scale=gain, bias=shift)
                 return
             activated = block_pool.tile([P, B], F32)
             if gate == GATE_G:
                 nc.scalar.activation(out=activated[:], in_=bank[:], func=ACT.Tanh, scale=gain, bias=shift)
-                nc.vector.tensor_tensor(out=cell_t[:, j, :], in0=cell_t[:, j, :], in1=activated[:], op=ALU.mult)
+                nc.vector.tensor_tensor(out=cell_i[:, j, :], in0=cell_i[:, j, :], in1=activated[:], op=ALU.mult)
             else:
                 nc.scalar.activation(out=activated[:], in_=bank[:], func=ACT.Sigmoid, scale=gain, bias=shift)
                 c_bank = psum_turn.tile([P, B], BF16, tag="turned")
                 for m in range(BATCH_TILES):
                     nc.tensor.transpose(c_bank[:, m * P : (m + 1) * P], c_sb[:, m, block], ident_bf16[:])
-                nc.vector.tensor_tensor(out=activated[:], in0=c_bank[:], in1=activated[:], op=ALU.mult)
-                nc.vector.tensor_tensor(out=cell_t[:, j, :], in0=cell_t[:, j, :], in1=activated[:], op=ALU.add)
+                nc.vector.tensor_tensor(out=cell_f[:, j, :], in0=c_bank[:], in1=activated[:], op=ALU.mult)
 
         def cell_back(m):
             row = {
@@ -274,9 +271,11 @@ def tile_hyperlstmcell_pb_kernel(
             for half in range(HALVES):
                 bank = psum_turn.tile([P, ROWS], F32, tag="turned")
                 for i in range(ROWS // P):
-                    nc.tensor.transpose(
-                        bank[:, i * P : (i + 1) * P], cell_t[:, half * (ROWS // P) + i, m * P : (m + 1) * P], ident_f32[:],
-                    )
+                    for term in (cell_i, cell_f):
+                        nc.tensor.matmul(
+                            out=bank[:, i * P : (i + 1) * P], lhsT=term[:, half * (ROWS // P) + i, m * P : (m + 1) * P],
+                            rhs=ident_f32[:], is_transpose=True, start=(term is cell_i), stop=(term is cell_f),
+                        )
                 nc.scalar.activation(
                     out=row["values"][:, half * ROWS : (half + 1) * ROWS], in_=bank[:], func=ACT.Identity,
                     accum_out=row["sums"][:, half : half + 1],
@@ -298,13 +297,23 @@ def tile_hyperlstmcell_pb_kernel(
         nc.vector.memset(ones[:], 1.0)
         bias_rows = keep.tile([P, (GATES - FIRST_BIAS_ROW_GATE) * H], BF16)
         nc.vector.memset(bias_rows[:], 0.0)
-        nc.sync.dma_start(out=bias_rows[0:1, :], in_=bias[FIRST_BIAS_ROW_GATE * H :].unsqueeze(0))
-        act_rows = {"x": load_rows(x), "h": load_rows(h)}
+        step_rows = {}
+
+        def load_step(q):
+            first_row = GATE_ORDER[q // (HALVES * STEPS_PER_HALF_GATE)] * H + (q // STEPS_PER_HALF_GATE) % HALVES * ROWS
+            matrix = big_weight[("x", "h")[(q % STEPS_PER_HALF_GATE) // PASSES]]
+            step_rows[q // PASSES] = load_rows(matrix[first_row : first_row + ROWS, :])
+
+        act_rows = {}
+        for i, (name, act) in enumerate((("x", x), ("h", h))):
+            act_rows[name] = load_rows(act)
+            load_step(PASSES * i)
         emb_rows = {}
         for name in ("x", "h", "b"):
             emb_rows[name] = pre_pool.tile([P, BATCH_TILES, GATES * E], BF16, name="emb_rows_" + name, tag="pre")
             nc.sync.dma_start(out=emb_rows[name][:], in_=embedding[name].rearrange("(m p) g e -> p m (g e)", p=P))
-        load_small_weights(0, gate_parts[0])
+            load_small_weight(0, name, gate_parts[0])
+        nc.sync.dma_start(out=bias_rows[0:1, :], in_=bias[FIRST_BIAS_ROW_GATE * H :].unsqueeze(0))
         vector_rows = const.tile([P, P], BF16)
         nc.vector.memset(vector_rows[:], 0.0)
         for first_row, vector in ((0, ln_gamma), (GATES * UNIT_BLOCKS, ln_beta)):
@@ -313,15 +322,35 @@ def tile_hyperlstmcell_pb_kernel(
                 in_=vector.rearrange("g (j p) -> (g j) p", p=P),
             )
 
+        step_grouped, half_gate_weights = {}, {}
+
+        def turn_step(q, vector_helps):
+            step_grouped[q] = turn(step_rows[q // PASSES], q % PASSES, vector_helps)
+
+        def quantise_step(q):
+            if q % STEPS_PER_HALF_GATE == 0:
+                weights = {}
+                for name in ("x", "h"):
+                    weights["codes_" + name] = half_gate.tile([P, PASSES, ROWS], U32, align_bytes=64, name="codes_" + name)
+                    weights["scales_" + name] = half_gate.tile([P, PASSES, ROWS], U8, align_bytes=64, name="scales_" + name)
+                half_gate_weights[q // STEPS_PER_HALF_GATE] = weights
+            weights = half_gate_weights[q // STEPS_PER_HALF_GATE]
+            name, g = ("x", "h")[(q % STEPS_PER_HALF_GATE) // PASSES], q % PASSES
+            quantise(step_grouped[q], weights["codes_" + name][:, g, :], weights["scales_" + name][:, g, :])
+
         act_codes, act_scales = {}, {}
-        for name in ("x", "h"):
+        for i, name in enumerate(("x", "h")):
             act_codes[name] = keep.tile([P, PASSES, B], U32, align_bytes=64, name="act_codes_" + name)
             act_scales[name] = keep.tile([P, PASSES, B], U8, align_bytes=64, name="act_scales_" + name)
             for g in range(PASSES):
                 quantise(turn(act_rows[name], g, True), act_codes[name][:, g, :], act_scales[name][:, g, :])
+            for q in range(PASSES * i, PASSES * (i + 1)):
+                turn_step(q, True)
+                quantise_step(q)
 
         emb_t = {}
-        for name in ("x", "h", "b"):
+
+        def turn_embedding(name):
             emb_t[name] = keep.tile([P, GATES, B], BF16, name="emb_t_" + name)
             for first_gate in range(0, GATES, 2):
                 transpose_eight(
@@ -334,17 +363,23 @@ def tile_hyperlstmcell_pb_kernel(
                 )
             turn_small_weight(name, gate_parts[0])
 
-        vector_bank = psum_turn.tile([P, P], BF16, tag="turned")
-        nc.tensor.transpose(vector_bank[:], vector_rows[:], ident_bf16[:])
+        for name in ("x", "h", "b"):
+            turn_embedding(name)
+
         unit_columns = const.tile([P, P], F32)
-        nc.scalar.copy(out=unit_columns[:], in_=vector_bank[:])
+
+        def turn_unit_columns():
+            vector_bank = psum_turn.tile([P, P], BF16, tag="turned")
+            nc.tensor.transpose(vector_bank[:], vector_rows[:], ident_bf16[:])
+            nc.scalar.copy(out=unit_columns[:], in_=vector_bank[:])
 
         c_sb = keep.tile([P, BATCH_TILES, H], BF16)
-        cell_t = keep.tile([P, UNIT_BLOCKS, B], F32)
+        cell_i = keep.tile([P, UNIT_BLOCKS, B], F32)
+        cell_f = keep.tile([P, UNIT_BLOCKS, B], F32)
         free_axis_vectors = {}
 
-        step_rows, step_grouped, half_gate_weights, tiles, rows, cell_state = {}, {}, {}, {}, {}, {}
-        for t in range(-(TURN_AHEAD + LOAD_AHEAD), N_TILES + LAST_LAG):
+        tiles, rows, cell_state = {}, {}, {}
+        for t in range(STEPS_PER_HALF_GATE - (TURN_AHEAD + LOAD_AHEAD), N_TILES + LAST_LAG):
             has_tile = 0 <= t < N_TILES
             row0, row1, row2 = [completed_row(t - lag) for lag in range(LAST_LAG + 1)]
 
@@ -352,27 +387,26 @@ def tile_hyperlstmcell_pb_kernel(
                 read_psum(t, tiles[t])
             if row1 is not None and GATE_ORDER[row1[0]] == GATE_O:
                 row = rows[row1]
-                row["scaled"] = scaled_pool.tile([P, H], F32, name="scaled")
-                centre_and_gain(row["scaled"][:], row["pre"][:], row["neg_mean"], free_axis_vectors["gain_o"][:])
+                centre_and_gain(row["pre"][:], row["pre"][:], row["neg_mean"], free_axis_vectors["gain_o"][:])
             if 0 <= t + 1 < N_TILES:
                 tiles[t + 1] = start_tile(t + 1)
 
             q = t + TURN_AHEAD + LOAD_AHEAD
-            if 0 <= q < N_STEPS and q % PASSES == 0:
-                first_row = GATE_ORDER[q // (HALVES * STEPS_PER_HALF_GATE)] * H + (q // STEPS_PER_HALF_GATE) % HALVES * ROWS
-                matrix = big_weight[("x", "h")[(q % STEPS_PER_HALF_GATE) // PASSES]]
-                step_rows[q // PASSES] = load_rows(matrix[first_row : first_row + ROWS, :])
+            if STEPS_PER_HALF_GATE <= q < N_STEPS and q % PASSES == 0:
+                load_step(q)
             q = t + TURN_AHEAD
-            if 0 <= q < N_STEPS:
-                step_grouped[q] = turn(step_rows[q // PASSES], q % PASSES, t < VECTOR_HELPS_UNTIL)
+            if STEPS_PER_HALF_GATE <= q < N_STEPS:
+                turn_step(q, t < VECTOR_HELPS_UNTIL)
 
             if has_tile and t // TILES_PER_GATE + 1 < GATES:
                 next_position, slot_in_gate = t // TILES_PER_GATE + 1, t % TILES_PER_GATE
                 if slot_in_gate == 0:
-                    load_small_weights(next_position, gate_parts[next_position])
+                    for name in ("x", "h", "b"):
+                        load_small_weight(next_position, name, gate_parts[next_position])
                 if slot_in_gate in (1, 2, 3):
                     turn_small_weight(("x", "h", "b")[slot_in_gate - 1], gate_parts[next_position])
             if t == 0:
+                turn_unit_columns()
                 nc.sync.dma_start(out=c_sb[:], in_=c.rearrange("(m p) n -> p m n", p=P))
                 for name, vector in (
                     ("gain_c", lnc_gamma), ("shift_c", lnc_beta),
@@ -384,16 +418,8 @@ def tile_hyperlstmcell_pb_kernel(
             if has_tile:
                 add_products(tiles[t])
             q = t + QUANTISE_AHEAD
-            if 0 <= q < N_STEPS:
-                if q % STEPS_PER_HALF_GATE == 0:
-                    weights = {}
-                    for name in ("x", "h"):
-                        weights["codes_" + name] = half_gate.tile([P, PASSES, ROWS], U32, align_bytes=64, name="codes_" + name)
-                        weights["scales_" + name] = half_gate.tile([P, PASSES, ROWS], U8, align_bytes=64, name="scales_" + name)
-                    half_gate_weights[q // STEPS_PER_HALF_GATE] = weights
-                weights = half_gate_weights[q // STEPS_PER_HALF_GATE]
-                name, g = ("x", "h")[(q % STEPS_PER_HALF_GATE) // PASSES], q % PASSES
-                quantise(step_grouped[q], weights["codes_" + name][:, g, :], weights["scales_" + name][:, g, :])
+            if STEPS_PER_HALF_GATE <= q < N_STEPS:
+                quantise_step(q)
             if has_tile:
                 finish_tile(t, tiles[t])
             if 0 <= t + 1 < N_TILES:
@@ -405,8 +431,8 @@ def tile_hyperlstmcell_pb_kernel(
             if row1 is not None:
                 row = rows[row1]
                 if GATE_ORDER[row1[0]] == GATE_O:
-                    scale_and_shift(row["scaled"][:], row["inv_std"], free_axis_vectors["shift_o"][:])
-                    nc.scalar.activation(out=row["scaled"][:], in_=row["scaled"][:], func=ACT.Sigmoid)
+                    scale_and_shift(row["pre"][:], row["inv_std"], free_axis_vectors["shift_o"][:])
+                    nc.scalar.activation(out=row["pre"][:], in_=row["pre"][:], func=ACT.Sigmoid)
                 else:
                     offset = stats.tile([P, 1], F32)
                     nc.gpsimd.tensor_tensor(out=offset[:], in0=row["neg_mean"][:], in1=row["inv_std"][:], op=ALU.mult)
@@ -432,5 +458,5 @@ def tile_hyperlstmcell_pb_kernel(
             if row2 is not None and GATE_ORDER[row2[0]] == GATE_O:
                 m = row2[1]
                 new_h = results.tile([P, H], F32, tag="result")
-                nc.vector.tensor_tensor(out=new_h[:], in0=rows[row2]["scaled"][:], in1=cell_state[m]["values"][:], op=ALU.mult)
+                nc.vector.tensor_tensor(out=new_h[:], in0=rows[row2]["pre"][:], in1=cell_state[m]["values"][:], op=ALU.mult)
                 nc.sync.dma_start(out=out_0[m * P : (m + 1) * P, :], in_=new_h[:])

@@ -38,6 +38,8 @@ TURN_AHEAD = QUANTISE_AHEAD + 1
 LOAD_AHEAD = 4
 LAST_LAG = 2
 UNIT_BLOCKS = H // P
+BIAS_COLUMN = 2 * GATES * UNIT_BLOCKS
+BROADCAST_SLOT = N_STEPS - TURN_AHEAD - LOAD_AHEAD + 1
 VECTOR_HELPS_UNTIL = 0
 BLOCKS_PER_SLOT = 2
 FIRST_BACK_SLOT = 1 + UNIT_BLOCKS // BLOCKS_PER_SLOT
@@ -176,8 +178,15 @@ def tile_hyperlstmcell_pb_kernel(
             tile["z_b"] = psum_out.tile([P, ROWS], F32, name="z_b")
             nc.tensor.matmul(
                 out=tile["z_b"][:], lhsT=emb_t["b"][:, gate, m * P : (m + 1) * P], rhs=gate_parts[position]["small_b"][:, units],
-                start=True, stop=(position == 0),
+                start=True, stop=False,
             )
+            if position == 0:
+                for i in range(ROWS // P):
+                    column = BIAS_COLUMN + half * (ROWS // P) + i
+                    nc.tensor.matmul(
+                        out=tile["z_b"][:, i * P : (i + 1) * P], lhsT=unit_columns[:, column : column + 1].to_broadcast([P, P]),
+                        rhs=ident_f32[:], is_transpose=True, start=False, stop=(i == ROWS // P - 1),
+                    )
             if position > 0:
                 first_unit = (gate - FIRST_BIAS_ROW_GATE) * H + half * ROWS
                 nc.tensor.matmul(
@@ -203,8 +212,6 @@ def tile_hyperlstmcell_pb_kernel(
                     "sums": sums_pool.tile([P, HALVES], F32, name="sums"),
                 }
             row = rows[position, m]
-            if position == 0:
-                nc.vector.tensor_tensor(out=tile["term_x"][:], in0=tile["term_x"][:], in1=first_bias[:, units], op=ALU.add)
             nc.vector.scalar_tensor_tensor(
                 out=row["pre"][:, units], in0=tile["z_b"][:], scalar=1.0, in1=tile["term_x"][:],
                 op0=ALU.mult, op1=ALU.add, accum_out=row["sums"][:, half : half + 1],
@@ -291,8 +298,6 @@ def tile_hyperlstmcell_pb_kernel(
             nc.scalar.activation(out=row["values"][:], in_=new_c[:], func=ACT.Tanh)
 
         gate_parts = {position: {} for position in range(GATES)}
-        first_bias = keep.tile([P, H], BF16)
-        nc.gpsimd.dma_start(out=first_bias[:], in_=bias[GATE_ORDER[0] * H : (GATE_ORDER[0] + 1) * H].partition_broadcast(P))
         ones = const.tile([P, P], BF16)
         nc.vector.memset(ones[:], 1.0)
         bias_rows = keep.tile([P, (GATES - FIRST_BIAS_ROW_GATE) * H], BF16)
@@ -321,6 +326,10 @@ def tile_hyperlstmcell_pb_kernel(
                 out=vector_rows[first_row : first_row + GATES * UNIT_BLOCKS, :],
                 in_=vector.rearrange("g (j p) -> (g j) p", p=P),
             )
+        nc.sync.dma_start(
+            out=vector_rows[BIAS_COLUMN : BIAS_COLUMN + UNIT_BLOCKS, :],
+            in_=bias[GATE_ORDER[0] * H : (GATE_ORDER[0] + 1) * H].rearrange("(j p) -> j p", p=P),
+        )
 
         step_grouped, half_gate_weights = {}, {}
 
@@ -367,11 +376,9 @@ def tile_hyperlstmcell_pb_kernel(
             turn_embedding(name)
 
         unit_columns = const.tile([P, P], F32)
-
-        def turn_unit_columns():
-            vector_bank = psum_turn.tile([P, P], BF16, tag="turned")
-            nc.tensor.transpose(vector_bank[:], vector_rows[:], ident_bf16[:])
-            nc.scalar.copy(out=unit_columns[:], in_=vector_bank[:])
+        vector_bank = psum_turn.tile([P, P], BF16, tag="turned")
+        nc.tensor.transpose(vector_bank[:], vector_rows[:], ident_bf16[:])
+        nc.scalar.copy(out=unit_columns[:], in_=vector_bank[:])
 
         c_sb = keep.tile([P, BATCH_TILES, H], BF16)
         cell_i = keep.tile([P, UNIT_BLOCKS, B], F32)
@@ -406,8 +413,8 @@ def tile_hyperlstmcell_pb_kernel(
                 if slot_in_gate in (1, 2, 3):
                     turn_small_weight(("x", "h", "b")[slot_in_gate - 1], gate_parts[next_position])
             if t == 0:
-                turn_unit_columns()
                 nc.sync.dma_start(out=c_sb[:], in_=c.rearrange("(m p) n -> p m n", p=P))
+            if t == BROADCAST_SLOT:
                 for name, vector in (
                     ("gain_c", lnc_gamma), ("shift_c", lnc_beta),
                     ("gain_o", ln_gamma[GATE_O, :]), ("shift_o", ln_beta[GATE_O, :]),

@@ -19,37 +19,50 @@ H = 1024
 E = 128
 GATES = 4
 BATCH_TILES = B // P
+PAIR = 2
+PAIRS = BATCH_TILES // PAIR
+SAMPLES = PAIR * P
 K_PASS = 4 * P
 PASSES = K // K_PASS
 ROWS = 512
 HALVES = H // ROWS
-TILES_PER_GATE = HALVES * BATCH_TILES
-N_TILES = GATES * TILES_PER_GATE
+UNIT_BLOCKS = H // P
+TILES_PER_GATE = HALVES * PAIR
+TILES_PER_PAIR = GATES * TILES_PER_GATE
+N_TILES = PAIRS * TILES_PER_PAIR
 EPS = 1e-6
 
 GATE_I, GATE_F, GATE_G, GATE_O = 0, 1, 2, 3
 GATE_ORDER = (GATE_I, GATE_G, GATE_F, GATE_O)
-FIRST_BIAS_ROW_GATE = 1
 
 STEPS_PER_HALF_GATE = 2 * PASSES
-N_STEPS = GATES * HALVES * STEPS_PER_HALF_GATE
-QUANTISE_AHEAD = STEPS_PER_HALF_GATE + 1
-TURN_AHEAD = QUANTISE_AHEAD + 1
-LOAD_AHEAD = 4
-LAST_LAG = 2
-UNIT_BLOCKS = H // P
+HALF_GATES = GATES * HALVES
+N_STEPS = HALF_GATES * STEPS_PER_HALF_GATE
+SCALE_ROWS = 4
+STEPS_PER_SLOT = STEPS_PER_HALF_GATE // PAIR
+TURN_LEAD = 1
+LOAD_LEAD = 1
+
 BIAS_COLUMN = 2 * GATES * UNIT_BLOCKS
-BROADCAST_SLOT = N_STEPS - TURN_AHEAD - LOAD_AHEAD + 1
-VECTOR_HELPS_UNTIL = 0
-BLOCKS_PER_SLOT = 2
-FIRST_BACK_SLOT = 1 + UNIT_BLOCKS // BLOCKS_PER_SLOT
-BACK_PER_SLOT = 2
+FIRST_BIAS_ROW_GATE = 1
+GATE_BANKS = UNIT_BLOCKS // 2
+BANKS_PER_SLOT = 2
 
 FLOPS = 2 * (2 * B * K * GATES * H) + 3 * (2 * B * E * GATES * H)
 
 
 def where(t):
-    return t // TILES_PER_GATE, (t % TILES_PER_GATE) // BATCH_TILES, t % BATCH_TILES
+    pair, rest = divmod(t, TILES_PER_PAIR)
+    position, place = divmod(rest, TILES_PER_GATE)
+    if pair == 0:
+        half, i = divmod(place, PAIR)
+    else:
+        i, half = divmod(place, HALVES)
+    return position, half, pair * PAIR + i
+
+
+def scale_row(name, g):
+    return SCALE_ROWS * (PASSES * ("x", "h").index(name) + g)
 
 
 def completed_row(t):
@@ -58,11 +71,37 @@ def completed_row(t):
     return None
 
 
+def quantise_slot(q):
+    return q // STEPS_PER_SLOT - 3
+
+
+def bank_slot(pair, position, k):
+    return pair * TILES_PER_PAIR + (position + 1) * TILES_PER_GATE + 2 + k // BANKS_PER_SLOT
+
+
+def back_slot(m):
+    pair, i = divmod(m, PAIR)
+    last = bank_slot(pair, GATE_ORDER.index(GATE_F), GATE_BANKS - 1)
+    return last + 2 + (i if pair < PAIRS - 1 else 0)
+
+
+def row_slot(position, m):
+    return [t for t in range(N_TILES) if completed_row(t) == (position, m)][0]
+
+
+def new_h_slot(m):
+    return max(back_slot(m), row_slot(GATES - 1, m)) + 3
+
+
+LAST_SLOT = new_h_slot(BATCH_TILES - 1)
+
+
 def tile_hyperlstmcell_pb_kernel(
     tc, x, h, c, emb_h, emb_x, emb_b, Wsh, Wsx, Wsb, Wih, Whh, bias,
     ln_gamma, ln_beta, lnc_gamma, lnc_beta, out_0, out_1,
 ):
     nc = tc.nc
+    activation = {"x": x, "h": h}
     big_weight = {"x": Wih, "h": Whh}
     small_weight = {"x": Wsx, "h": Wsh, "b": Wsb}
     embedding = {"x": emb_x, "h": emb_h, "b": emb_b}
@@ -70,20 +109,18 @@ def tile_hyperlstmcell_pb_kernel(
     with ExitStack() as ctx:
         const = ctx.enter_context(tc.tile_pool(name="const", bufs=1))
         keep = ctx.enter_context(tc.tile_pool(name="keep", bufs=1))
-        big_rows = ctx.enter_context(tc.tile_pool(name="big_rows", bufs=3))
+        big_rows = ctx.enter_context(tc.tile_pool(name="big_rows", bufs=2))
         small_rows = ctx.enter_context(tc.tile_pool(name="small_rows", bufs=3))
         grouped_pool = ctx.enter_context(tc.tile_pool(name="grouped", bufs=3))
-        half_gate = ctx.enter_context(tc.tile_pool(name="half_gate", bufs=2))
-        per_gate = ctx.enter_context(tc.tile_pool(name="per_gate", bufs=2))
         work = ctx.enter_context(tc.tile_pool(name="work", bufs=2))
         z_pool = ctx.enter_context(tc.tile_pool(name="z_sb", bufs=2))
-        pre_pool = ctx.enter_context(tc.tile_pool(name="pre", bufs=8))
-        sums_pool = ctx.enter_context(tc.tile_pool(name="sums", bufs=6))
-        block_pool = ctx.enter_context(tc.tile_pool(name="block", bufs=3))
-        cell_rows = ctx.enter_context(tc.tile_pool(name="cell_rows", bufs=BATCH_TILES))
-        scratch = ctx.enter_context(tc.tile_pool(name="scratch", bufs=2))
-        results = ctx.enter_context(tc.tile_pool(name="results", bufs=2))
-        stats = ctx.enter_context(tc.tile_pool(name="stats", bufs=4))
+        pre_pool = ctx.enter_context(tc.tile_pool(name="pre", bufs=5))
+        sums_pool = ctx.enter_context(tc.tile_pool(name="sums", bufs=8))
+        block_pool = ctx.enter_context(tc.tile_pool(name="block", bufs=2))
+        cell_rows = ctx.enter_context(tc.tile_pool(name="cell_rows", bufs=PAIR))
+        results = ctx.enter_context(tc.tile_pool(name="results", bufs=1))
+        scratch = ctx.enter_context(tc.tile_pool(name="scratch", bufs=1))
+        stats = ctx.enter_context(tc.tile_pool(name="stats", bufs=8))
         psum_out = ctx.enter_context(tc.psum_pool(name="psum_out", bufs=1))
         psum_turn = ctx.enter_context(tc.psum_pool(name="psum_turn", bufs=3))
 
@@ -96,374 +133,436 @@ def tile_hyperlstmcell_pb_kernel(
         exp_minus_one = const.tile([P, 1], F32)
         nc.vector.memset(exp_minus_one[:], -1.0)
 
-        def load_rows(dram_rows):
-            rows_sb = big_rows.tile([P, ROWS // P, K], BF16)
-            nc.sync.dma_start(out=rows_sb[:], in_=dram_rows.rearrange("(r p) k -> p r k", p=P))
-            return rows_sb
+        tiles, rows, cells, step_rows, step_grouped = {}, {}, {}, {}, {}
+        act_rows, emb_rows, c_rows, emb_t, small_t, unit_vectors = {}, {}, {}, {}, {}, {}
+        codes, scales = {}, {}
 
-        def turn(rows_sb, g, vector_helps):
-            grouped = grouped_pool.tile([P, 4 * ROWS], BF16, align_bytes=64)
-            grouped_words = grouped[:].bitcast(F32).rearrange("p (r u) -> p r u", u=2)
-            for pair in range(2):
-                bank = psum_turn.tile([P, 2, 2 * P], F32, tag="turned")
-                for u in range(2):
-                    for r in range(2):
-                        words = slice(2 * P * g + u, 2 * P * (g + 1), 2)
-                        nc.tensor.transpose(
-                            bank[:, u, r * P : (r + 1) * P],
-                            rows_sb[:, 2 * pair + r, :].bitcast(F32)[:, words],
-                            ident_f32[:],
-                        )
-                target = grouped_words[:, 2 * P * pair : 2 * P * (pair + 1), :]
-                if vector_helps and pair == 1:
-                    nc.vector.tensor_copy(out=target, in_=bank[:].rearrange("p u r -> p r u"))
-                else:
-                    nc.scalar.copy(out=target, in_=bank[:].rearrange("p u r -> p r u"))
-            return grouped
-
-        def quantise(grouped, codes, scales):
-            nc.vector.quantize_mx(out=codes.bitcast(FP8X4), scales=scales, in_=grouped[:])
-
-        def transpose_eight(blocks, dst):
-            bank = psum_turn.tile([P, 8 * P], BF16, tag="turned")
-            for i, block in enumerate(blocks):
-                nc.tensor.transpose(bank[:, i * P : (i + 1) * P], block, ident_bf16[:])
-            nc.scalar.copy(out=dst, in_=bank[:])
-
-        def load_small_weight(position, name, parts):
-            gate = GATE_ORDER[position]
-            parts["rows_" + name] = small_rows.tile([P, H // P, E], BF16, name="rows_" + name, tag="rows")
+        def load_act(name, pair):
+            act_rows[name] = pre_pool.tile([P, PAIR, K], BF16, name="act_rows_" + name, tag="pre")
             nc.sync.dma_start(
-                out=parts["rows_" + name][:], in_=small_weight[name][gate].rearrange("(j p) e -> p j e", p=P)
+                out=act_rows[name][:],
+                in_=activation[name][pair * SAMPLES : (pair + 1) * SAMPLES, :].rearrange("(r p) k -> p r k", p=P),
             )
 
-        def turn_small_weight(name, parts):
-            parts["small_" + name] = per_gate.tile([P, H], BF16, name="small_" + name)
-            transpose_eight([parts["rows_" + name][:, j, :] for j in range(H // P)], parts["small_" + name][:])
+        def load_embedding(name, pair):
+            emb_rows[name] = pre_pool.tile([P, PAIR, GATES * E], BF16, name="emb_rows_" + name, tag="pre")
+            nc.sync.dma_start(
+                out=emb_rows[name][:],
+                in_=embedding[name][pair * SAMPLES : (pair + 1) * SAMPLES].rearrange("(m p) g e -> p m (g e)", p=P),
+            )
 
-        def start_tile(t):
+        def load_step(q):
+            half_gate, name = q // STEPS_PER_HALF_GATE, ("x", "h")[(q % STEPS_PER_HALF_GATE) // PASSES]
+            first_row = GATE_ORDER[half_gate // HALVES] * H + half_gate % HALVES * ROWS
+            step_rows[q // PASSES] = big_rows.tile([P, ROWS // P, K], BF16, name="big")
+            nc.sync.dma_start(
+                out=step_rows[q // PASSES][:],
+                in_=big_weight[name][first_row : first_row + ROWS, :].rearrange("(r p) k -> p r k", p=P),
+            )
+
+        def load_small_weight(position, name):
+            small_t[position, name] = small_rows.tile([P, UNIT_BLOCKS, E], BF16, name="small_rows")
+            nc.sync.dma_start(
+                out=small_t[position, name][:],
+                in_=small_weight[name][GATE_ORDER[position]].rearrange("(j p) e -> p j e", p=P),
+            )
+
+        def turn_rows(rows_sb, first, g, grouped, pair, on_vector):
+            bank = psum_turn.tile([P, 2, 2 * P], F32, tag="turned", name="turned_rows")
+            for u in range(2):
+                for r in range(2):
+                    words = slice(2 * P * g + u, 2 * P * (g + 1), 2)
+                    nc.tensor.transpose(
+                        bank[:, u, r * P : (r + 1) * P], rows_sb[:, first + r, :].bitcast(F32)[:, words], ident_f32[:],
+                    )
+            target = grouped[:].bitcast(F32).rearrange("p (r u) -> p r u", u=2)[:, 2 * P * pair : 2 * P * (pair + 1), :]
+            if on_vector:
+                nc.vector.tensor_copy(out=target, in_=bank[:].rearrange("p u r -> p r u"))
+            else:
+                nc.scalar.copy(out=target, in_=bank[:].rearrange("p u r -> p r u"))
+
+        for name in ("x", "h"):
+            codes["act", name] = keep.tile([P, PASSES, B], U32, align_bytes=64, name="act_codes_" + name)
+        scales["act"] = keep.tile([P, B], U8, align_bytes=64, name="act_scales")
+
+        def turn_act(name, g, on_vector):
+            grouped = grouped_pool.tile([P, 4 * SAMPLES], BF16, align_bytes=64, name="act_grouped", tag="grouped")
+            turn_rows(act_rows[name], 0, g, grouped, 0, on_vector)
+            return grouped
+
+        def quantise_act(name, pair, g, grouped):
+            samples = slice(pair * SAMPLES, (pair + 1) * SAMPLES)
+            nc.vector.quantize_mx(
+                out=codes["act", name][:, g, samples].bitcast(FP8X4), scales=scales["act"][scale_row(name, g) : P, samples],
+                in_=grouped[:],
+            )
+
+        def turn_step(q, pair, on_vector):
+            if pair == 0:
+                step_grouped[q] = grouped_pool.tile([P, 4 * ROWS], BF16, align_bytes=64, name="grouped")
+            turn_rows(step_rows[q // PASSES], 2 * pair, q % PASSES, step_grouped[q], pair, on_vector)
+
+        def quantise_step(q):
+            half_gate, name, g = q // STEPS_PER_HALF_GATE, ("x", "h")[(q % STEPS_PER_HALF_GATE) // PASSES], q % PASSES
+            if g == 0:
+                codes[half_gate, name] = keep.tile([P, PASSES, ROWS], U32, align_bytes=64, name="codes_%s_%d" % (name, half_gate))
+            if q % STEPS_PER_HALF_GATE == 0:
+                scales[half_gate] = keep.tile([P, ROWS], U8, align_bytes=64, name="scales_%d" % half_gate)
+            nc.vector.quantize_mx(
+                out=codes[half_gate, name][:, g, :].bitcast(FP8X4),
+                scales=scales[half_gate][scale_row(name, g) : P, :],
+                in_=step_grouped[q][:],
+            )
+
+        def transpose_eight(blocks, dst, **shape):
+            bank = psum_turn.tile([P, 8 * P], BF16, tag="turned", name="turned_eight")
+            for i, block in enumerate(blocks):
+                nc.tensor.transpose(bank[:, i * P : (i + 1) * P], block, ident_bf16[:])
+            nc.scalar.copy(out=dst, in_=bank[:].rearrange("p (g b) -> p g b", **shape) if shape else bank[:])
+
+        for name in ("x", "h", "b"):
+            emb_t[name] = keep.tile([P, GATES, B], BF16, name="emb_t_" + name)
+
+        def turn_embedding(name, pair):
+            transpose_eight(
+                [emb_rows[name][:, i, gate * E : (gate + 1) * E] for gate in range(GATES) for i in range(PAIR)],
+                emb_t[name][:, :, pair * SAMPLES : (pair + 1) * SAMPLES], g=GATES,
+            )
+
+        def turn_small_weight(position, name):
+            rows_sb = small_t[position, name]
+            small_t[position, name] = keep.tile([P, H], BF16, name="small_%s_%d" % (name, position))
+            transpose_eight([rows_sb[:, j, :] for j in range(UNIT_BLOCKS)], small_t[position, name][:])
+
+        def start_z(t, name):
             position, half, m = where(t)
-            gate = GATE_ORDER[position]
+            z = tiles.setdefault(t, {})["z_" + name] = psum_out.tile([P, ROWS], F32, name="z_" + name)
+            nc.tensor.matmul(
+                out=z[:], lhsT=emb_t[name][:, GATE_ORDER[position], m * P : (m + 1) * P],
+                rhs=small_t[position, name][:, half * ROWS : (half + 1) * ROWS], start=True, stop=True,
+            )
+
+        def copy_z(t, name):
+            tile = tiles[t]
+            tile["z_sb_" + name] = z_pool.tile([P, ROWS], F32, name="z_sb_" + name)
+            nc.scalar.copy(out=tile["z_sb_" + name][:], in_=tile["z_" + name][:])
+
+        def start_products(t):
+            position, half, m = where(t)
             samples = slice(m * P, (m + 1) * P)
-            units = slice(half * ROWS, (half + 1) * ROWS)
-            parts = gate_parts[position]
-            weights = half_gate_weights[t // BATCH_TILES]
-            tile = {}
+            half_gate = HALVES * position + half
             for name in ("x", "h"):
-                tile["z_" + name] = psum_out.tile([P, ROWS], F32, name="z_" + name)
-                nc.tensor.matmul(
-                    out=tile["z_" + name][:], lhsT=emb_t[name][:, gate, samples], rhs=parts["small_" + name][:, units],
-                    start=True, stop=True,
-                )
-            for name in ("x", "h"):
-                tile["z_sb_" + name] = z_pool.tile([P, ROWS], F32, name="z_sb_" + name)
-                nc.scalar.copy(out=tile["z_sb_" + name][:], in_=tile["z_" + name][:])
-                tile["product_" + name] = psum_out.tile([P, ROWS], F32, name="product_" + name)
+                product = tiles[t]["product_" + name] = psum_out.tile([P, ROWS], F32, name="product_" + name)
                 for g in range(PASSES):
                     nc.tensor.matmul_mx(
-                        out=tile["product_" + name][:],
-                        lhsT=act_codes[name][:, g, samples].bitcast(FP8X4),
-                        lhsT_scale=act_scales[name][:, g, samples],
-                        rhs=weights["codes_" + name][:, g, :].bitcast(FP8X4),
-                        rhs_scale=weights["scales_" + name][:, g, :],
+                        out=product[:],
+                        lhsT=codes["act", name][:, g, samples].bitcast(FP8X4),
+                        lhsT_scale=scales["act"][scale_row(name, g) : P, samples],
+                        rhs=codes[half_gate, name][:, g, :].bitcast(FP8X4),
+                        rhs_scale=scales[half_gate][scale_row(name, g) : P, :],
                         start=(g == 0),
                         stop=(g == PASSES - 1),
                     )
-            return tile
 
-        def start_offset(t, tile):
+        def start_offset(t):
             position, half, m = where(t)
-            gate = GATE_ORDER[position]
-            units = slice(half * ROWS, (half + 1) * ROWS)
-            tile["z_b"] = psum_out.tile([P, ROWS], F32, name="z_b")
+            z_b = tiles[t]["z_b"] = psum_out.tile([P, ROWS], F32, name="z_b")
             nc.tensor.matmul(
-                out=tile["z_b"][:], lhsT=emb_t["b"][:, gate, m * P : (m + 1) * P], rhs=gate_parts[position]["small_b"][:, units],
-                start=True, stop=False,
+                out=z_b[:], lhsT=emb_t["b"][:, GATE_ORDER[position], m * P : (m + 1) * P],
+                rhs=small_t[position, "b"][:, half * ROWS : (half + 1) * ROWS], start=True, stop=False,
             )
-            if position == 0:
-                for i in range(ROWS // P):
-                    column = BIAS_COLUMN + half * (ROWS // P) + i
-                    nc.tensor.matmul(
-                        out=tile["z_b"][:, i * P : (i + 1) * P], lhsT=unit_columns[:, column : column + 1].to_broadcast([P, P]),
-                        rhs=ident_f32[:], is_transpose=True, start=False, stop=(i == ROWS // P - 1),
-                    )
+
+        def add_bias(t):
+            position, half, m = where(t)
+            gate, z_b = GATE_ORDER[position], tiles[t]["z_b"]
             if position > 0:
                 first_unit = (gate - FIRST_BIAS_ROW_GATE) * H + half * ROWS
                 nc.tensor.matmul(
-                    out=tile["z_b"][:], lhsT=ones[:], rhs=bias_rows[:, first_unit : first_unit + ROWS], start=False, stop=True,
+                    out=z_b[:], lhsT=ones[:], rhs=bias_rows[:, first_unit : first_unit + ROWS], start=False, stop=True,
+                )
+                return
+            for i in range(ROWS // P):
+                column = BIAS_COLUMN + half * (ROWS // P) + i
+                nc.tensor.matmul(
+                    out=z_b[:, i * P : (i + 1) * P], lhsT=unit_columns[:, column : column + 1].to_broadcast([P, P]),
+                    rhs=ident_f32[:], is_transpose=True, start=False, stop=(i == ROWS // P - 1),
                 )
 
-        def read_psum(t, tile):
-            for name in ("x", "h"):
-                tile["term_" + name] = work.tile([P, ROWS], F32, name="term_" + name)
-                nc.vector.tensor_tensor(
-                    out=tile["term_" + name][:], in0=tile["product_" + name][:], in1=tile["z_sb_" + name][:], op=ALU.mult,
-                )
+        def multiply(t, name):
+            tile = tiles[t]
+            tile["term_" + name] = work.tile([P, ROWS], F32, name="term_" + name)
+            nc.vector.tensor_tensor(
+                out=tile["term_" + name][:], in0=tile["product_" + name][:], in1=tile["z_sb_" + name][:], op=ALU.mult,
+            )
 
-        def add_products(tile):
+        def add_products(t):
+            tile = tiles[t]
             nc.vector.tensor_tensor(out=tile["term_x"][:], in0=tile["term_x"][:], in1=tile["term_h"][:], op=ALU.add)
 
-        def finish_tile(t, tile):
+        def finish_tile(t):
             position, half, m = where(t)
-            units = slice(half * ROWS, (half + 1) * ROWS)
             if half == 0:
                 rows[position, m] = {
-                    "pre": pre_pool.tile([P, H], F32, name="pre"),
-                    "sums": sums_pool.tile([P, HALVES], F32, name="sums"),
+                    "values": pre_pool.tile([P, H], F32, name="pre"), "sums": sums_pool.tile([P, HALVES], F32, name="sums"),
                 }
             row = rows[position, m]
             nc.vector.scalar_tensor_tensor(
-                out=row["pre"][:, units], in0=tile["z_b"][:], scalar=1.0, in1=tile["term_x"][:],
-                op0=ALU.mult, op1=ALU.add, accum_out=row["sums"][:, half : half + 1],
+                out=row["values"][:, half * ROWS : (half + 1) * ROWS], in0=tiles[t]["z_b"][:], scalar=1.0,
+                in1=tiles[t]["term_x"][:], op0=ALU.mult, op1=ALU.add, accum_out=row["sums"][:, half : half + 1],
             )
 
-        def start_stats(values, sums):
-            neg_mean = stats.tile([P, 1], F32)
+        def start_stats(row):
+            neg_mean = row["neg_mean"] = stats.tile([P, 1], F32, name="neg_mean")
             nc.gpsimd.tensor_scalar(
-                out=neg_mean[:], in0=sums[:, 0:1], scalar1=sums[:, 1:2], scalar2=-1.0 / H, op0=ALU.add, op1=ALU.mult,
+                out=neg_mean[:], in0=row["sums"][:, 0:1], scalar1=row["sums"][:, 1:2], scalar2=-1.0 / H,
+                op0=ALU.add, op1=ALU.mult,
             )
-            squares = scratch.tile([P, H], BF16)
-            sum_sq = stats.tile([P, 1], F32)
+            squares = scratch.tile([P, H], BF16, name="squares")
+            sum_sq = stats.tile([P, 1], F32, name="sum_sq")
             nc.scalar.activation(
-                out=squares[:], in_=values, func=ACT.Square, bias=neg_mean[:, 0:1], scale=1.0, accum_out=sum_sq[:],
+                out=squares[:], in_=row["values"][:], func=ACT.Square, bias=neg_mean[:, 0:1], scale=1.0, accum_out=sum_sq[:],
             )
-            root = stats.tile([P, 1], F32)
+            root = stats.tile([P, 1], F32, name="root")
             nc.gpsimd.tensor_tensor(out=root[:], in0=sum_sq[:], in1=exp_half[:], op=ALU.pow)
-            std_eps = stats.tile([P, 1], F32)
+            std_eps = stats.tile([P, 1], F32, name="std_eps")
             nc.gpsimd.tensor_scalar(
                 out=std_eps[:], in0=root[:], scalar1=1.0 / math.sqrt(H - 1), scalar2=EPS, op0=ALU.mult, op1=ALU.add,
             )
-            inv_std = stats.tile([P, 1], F32)
-            nc.gpsimd.tensor_tensor(out=inv_std[:], in0=std_eps[:], in1=exp_minus_one[:], op=ALU.pow)
-            return neg_mean, inv_std
+            row["inv_std"] = stats.tile([P, 1], F32, name="inv_std")
+            nc.gpsimd.tensor_tensor(out=row["inv_std"][:], in0=std_eps[:], in1=exp_minus_one[:], op=ALU.pow)
 
-        def centre_and_gain(out, values, neg_mean, gain):
-            nc.vector.scalar_tensor_tensor(
-                out=out, in0=values, scalar=neg_mean[:, 0:1], in1=gain, op0=ALU.add, op1=ALU.mult,
+        def normalise(row):
+            nc.vector.tensor_scalar(
+                out=row["values"][:], in0=row["values"][:], scalar1=row["neg_mean"][:, 0:1], scalar2=row["inv_std"][:, 0:1],
+                op0=ALU.add, op1=ALU.mult,
             )
 
-        def scale_and_shift(values, inv_std, shift):
-            nc.vector.scalar_tensor_tensor(
-                out=values, in0=values, scalar=inv_std[:, 0:1], in1=shift, op0=ALU.mult, op1=ALU.add,
-            )
-
-        def gate_block(position, j):
+        def gate_bank(pair, position, k):
             gate = GATE_ORDER[position]
-            block = slice(j * P, (j + 1) * P)
-            bank = psum_turn.tile([P, B], F32, tag="turned")
-            for m in range(BATCH_TILES):
-                nc.tensor.transpose(bank[:, m * P : (m + 1) * P], rows[position, m]["pre"][:, block], ident_f32[:])
-            column = gate * UNIT_BLOCKS + j
-            gain = unit_columns[:, column : column + 1]
-            shift = unit_columns[:, GATES * UNIT_BLOCKS + column : GATES * UNIT_BLOCKS + column + 1]
+            bank = psum_turn.tile([P, 2, SAMPLES], F32, tag="turned", name="turned_gate")
+            for i in range(2):
+                for s in range(PAIR):
+                    nc.tensor.transpose(
+                        bank[:, i, s * P : (s + 1) * P],
+                        rows[position, PAIR * pair + s]["values"][:, (2 * k + i) * P : (2 * k + i + 1) * P], ident_f32[:],
+                    )
             if gate == GATE_I:
-                nc.scalar.activation(out=cell_i[:, j, :], in_=bank[:], func=ACT.Sigmoid, scale=gain, bias=shift)
-                return
-            activated = block_pool.tile([P, B], F32)
-            if gate == GATE_G:
-                nc.scalar.activation(out=activated[:], in_=bank[:], func=ACT.Tanh, scale=gain, bias=shift)
-                nc.vector.tensor_tensor(out=cell_i[:, j, :], in0=cell_i[:, j, :], in1=activated[:], op=ALU.mult)
+                target = cell_i[:, 2 * k : 2 * k + 2, :]
             else:
-                nc.scalar.activation(out=activated[:], in_=bank[:], func=ACT.Sigmoid, scale=gain, bias=shift)
-                c_bank = psum_turn.tile([P, B], BF16, tag="turned")
-                for m in range(BATCH_TILES):
-                    nc.tensor.transpose(c_bank[:, m * P : (m + 1) * P], c_sb[:, m, block], ident_bf16[:])
-                nc.vector.tensor_tensor(out=cell_f[:, j, :], in0=c_bank[:], in1=activated[:], op=ALU.mult)
+                activated[position, k] = block_pool.tile([P, 2, SAMPLES], F32, name="activated")
+                target = activated[position, k][:]
+            for i in range(2):
+                column = gate * UNIT_BLOCKS + 2 * k + i
+                nc.scalar.activation(
+                    out=target[:, i, :], in_=bank[:, i, :], func=ACT.Tanh if gate == GATE_G else ACT.Sigmoid,
+                    scale=unit_columns[:, column : column + 1],
+                    bias=unit_columns[:, GATES * UNIT_BLOCKS + column : GATES * UNIT_BLOCKS + column + 1],
+                )
+
+        def gate_product(pair, position, k):
+            gate = GATE_ORDER[position]
+            blocks = slice(2 * k, 2 * k + 2)
+            if gate == GATE_G:
+                nc.vector.tensor_tensor(
+                    out=cell_i[:, blocks, :], in0=cell_i[:, blocks, :], in1=activated[position, k][:], op=ALU.mult,
+                )
+            if gate == GATE_F:
+                c_bank = psum_turn.tile([P, 2, SAMPLES], BF16, tag="turned", name="turned_c")
+                for i in range(2):
+                    for s in range(PAIR):
+                        nc.tensor.transpose(
+                            c_bank[:, i, s * P : (s + 1) * P], c_rows[pair][:, s, (2 * k + i) * P : (2 * k + i + 1) * P],
+                            ident_bf16[:],
+                        )
+                nc.vector.tensor_tensor(out=cell_f[:, blocks, :], in0=c_bank[:], in1=activated[position, k][:], op=ALU.mult)
 
         def cell_back(m):
-            row = {
-                "values": cell_rows.tile([P, H], F32, name="cell_row"),
-                "sums": sums_pool.tile([P, HALVES], F32, name="cell_sums"),
+            row = cells[m] = {
+                "values": cell_rows.tile([P, H], F32, name="cell_row"), "sums": sums_pool.tile([P, HALVES], F32, name="cell_sums"),
             }
             for half in range(HALVES):
-                bank = psum_turn.tile([P, ROWS], F32, tag="turned")
+                bank = psum_turn.tile([P, ROWS], F32, tag="turned", name="turned_cell")
                 for i in range(ROWS // P):
                     for term in (cell_i, cell_f):
                         nc.tensor.matmul(
-                            out=bank[:, i * P : (i + 1) * P], lhsT=term[:, half * (ROWS // P) + i, m * P : (m + 1) * P],
+                            out=bank[:, i * P : (i + 1) * P],
+                            lhsT=term[:, half * (ROWS // P) + i, m % PAIR * P : (m % PAIR + 1) * P],
                             rhs=ident_f32[:], is_transpose=True, start=(term is cell_i), stop=(term is cell_f),
                         )
                 nc.scalar.activation(
                     out=row["values"][:, half * ROWS : (half + 1) * ROWS], in_=bank[:], func=ACT.Identity,
                     accum_out=row["sums"][:, half : half + 1],
                 )
-            row["neg_mean"], row["inv_std"] = start_stats(row["values"][:], row["sums"])
-            return row
 
-        def finish_cell(m, row):
-            new_c = results.tile([P, H], F32, tag="result")
-            centre_and_gain(new_c[:], row["values"][:], row["neg_mean"], free_axis_vectors["gain_c"][:])
-            scale_and_shift(new_c[:], row["inv_std"], free_axis_vectors["shift_c"][:])
+        def apply_norm(out, row, gain, shift):
+            nc.vector.scalar_tensor_tensor(
+                out=out, in0=row["values"][:], scalar=row["neg_mean"][:, 0:1], in1=unit_vectors[gain][:],
+                op0=ALU.add, op1=ALU.mult,
+            )
+            nc.vector.scalar_tensor_tensor(
+                out=out, in0=out, scalar=row["inv_std"][:, 0:1], in1=unit_vectors[shift][:], op0=ALU.mult, op1=ALU.add,
+            )
+
+        def finish_cell(m):
+            new_c = results.tile([P, H], F32, name="new_c")
+            apply_norm(new_c[:], cells[m], "gain_c", "shift_c")
             nc.sync.dma_start(out=out_1[m * P : (m + 1) * P, :], in_=new_c[:])
-            nc.scalar.activation(out=row["values"][:], in_=new_c[:], func=ACT.Tanh)
+            nc.scalar.activation(out=cells[m]["values"][:], in_=new_c[:], func=ACT.Tanh)
 
-        gate_parts = {position: {} for position in range(GATES)}
-        ones = const.tile([P, P], BF16)
-        nc.vector.memset(ones[:], 1.0)
-        bias_rows = keep.tile([P, (GATES - FIRST_BIAS_ROW_GATE) * H], BF16)
-        nc.vector.memset(bias_rows[:], 0.0)
-        step_rows = {}
+        def finish_h(m):
+            values = cells[m]["values"]
+            nc.vector.tensor_tensor(out=values[:], in0=rows[GATES - 1, m]["values"][:], in1=values[:], op=ALU.mult)
+            nc.sync.dma_start(out=out_0[m * P : (m + 1) * P, :], in_=values[:])
 
-        def load_step(q):
-            first_row = GATE_ORDER[q // (HALVES * STEPS_PER_HALF_GATE)] * H + (q // STEPS_PER_HALF_GATE) % HALVES * ROWS
-            matrix = big_weight[("x", "h")[(q % STEPS_PER_HALF_GATE) // PASSES]]
-            step_rows[q // PASSES] = load_rows(matrix[first_row : first_row + ROWS, :])
 
-        act_rows = {}
-        for i, (name, act) in enumerate((("x", x), ("h", h))):
-            act_rows[name] = load_rows(act)
+        activated = {}
+        cell_i = keep.tile([P, UNIT_BLOCKS, SAMPLES], F32)
+        cell_f = keep.tile([P, UNIT_BLOCKS, SAMPLES], F32)
+        for i, name in enumerate(("x", "h")):
+            load_act(name, 0)
             load_step(PASSES * i)
-        emb_rows = {}
         for name in ("x", "h", "b"):
-            emb_rows[name] = pre_pool.tile([P, BATCH_TILES, GATES * E], BF16, name="emb_rows_" + name, tag="pre")
-            nc.sync.dma_start(out=emb_rows[name][:], in_=embedding[name].rearrange("(m p) g e -> p m (g e)", p=P))
-            load_small_weight(0, name, gate_parts[0])
-        nc.sync.dma_start(out=bias_rows[0:1, :], in_=bias[FIRST_BIAS_ROW_GATE * H :].unsqueeze(0))
+            load_embedding(name, 0)
+            load_small_weight(0, name)
         vector_rows = const.tile([P, P], BF16)
         nc.vector.memset(vector_rows[:], 0.0)
-        for first_row, vector in ((0, ln_gamma), (GATES * UNIT_BLOCKS, ln_beta)):
+        for i, vector in enumerate((ln_gamma, ln_beta)):
             nc.sync.dma_start(
-                out=vector_rows[first_row : first_row + GATES * UNIT_BLOCKS, :],
+                out=vector_rows[i * GATES * UNIT_BLOCKS : (i + 1) * GATES * UNIT_BLOCKS, :],
                 in_=vector.rearrange("g (j p) -> (g j) p", p=P),
             )
         nc.sync.dma_start(
             out=vector_rows[BIAS_COLUMN : BIAS_COLUMN + UNIT_BLOCKS, :],
             in_=bias[GATE_ORDER[0] * H : (GATE_ORDER[0] + 1) * H].rearrange("(j p) -> j p", p=P),
         )
+        ones = const.tile([P, P], BF16)
+        nc.vector.memset(ones[:], 1.0)
+        bias_rows = keep.tile([P, (GATES - FIRST_BIAS_ROW_GATE) * H], BF16)
+        nc.vector.memset(bias_rows[:], 0.0)
+        nc.sync.dma_start(out=bias_rows[0:1, :], in_=bias[FIRST_BIAS_ROW_GATE * H :].unsqueeze(0))
 
-        step_grouped, half_gate_weights = {}, {}
-
-        def turn_step(q, vector_helps):
-            step_grouped[q] = turn(step_rows[q // PASSES], q % PASSES, vector_helps)
-
-        def quantise_step(q):
-            if q % STEPS_PER_HALF_GATE == 0:
-                weights = {}
-                for name in ("x", "h"):
-                    weights["codes_" + name] = half_gate.tile([P, PASSES, ROWS], U32, align_bytes=64, name="codes_" + name)
-                    weights["scales_" + name] = half_gate.tile([P, PASSES, ROWS], U8, align_bytes=64, name="scales_" + name)
-                half_gate_weights[q // STEPS_PER_HALF_GATE] = weights
-            weights = half_gate_weights[q // STEPS_PER_HALF_GATE]
-            name, g = ("x", "h")[(q % STEPS_PER_HALF_GATE) // PASSES], q % PASSES
-            quantise(step_grouped[q], weights["codes_" + name][:, g, :], weights["scales_" + name][:, g, :])
-
-        act_codes, act_scales = {}, {}
+        waiting = []
         for i, name in enumerate(("x", "h")):
-            act_codes[name] = keep.tile([P, PASSES, B], U32, align_bytes=64, name="act_codes_" + name)
-            act_scales[name] = keep.tile([P, PASSES, B], U8, align_bytes=64, name="act_scales_" + name)
             for g in range(PASSES):
-                quantise(turn(act_rows[name], g, True), act_codes[name][:, g, :], act_scales[name][:, g, :])
+                grouped = turn_act(name, g, g == 1)
+                waiting.append((quantise_act, (name, 0, g, grouped)))
             for q in range(PASSES * i, PASSES * (i + 1)):
-                turn_step(q, True)
-                quantise_step(q)
-
-        emb_t = {}
-
-        def turn_embedding(name):
-            emb_t[name] = keep.tile([P, GATES, B], BF16, name="emb_t_" + name)
-            for first_gate in range(0, GATES, 2):
-                transpose_eight(
-                    [
-                        emb_rows[name][:, m, gate * E : (gate + 1) * E]
-                        for gate in (first_gate, first_gate + 1)
-                        for m in range(BATCH_TILES)
-                    ],
-                    emb_t[name][:, first_gate : first_gate + 2, :].rearrange("p g b -> p (g b)"),
-                )
-            turn_small_weight(name, gate_parts[0])
-
+                for pair in range(2):
+                    turn_step(q, pair, pair == 1)
+                waiting.append((quantise_step, (q,)))
+                while len(waiting) > 1:
+                    function, arguments = waiting.pop(0)
+                    function(*arguments)
+        for function, arguments in waiting:
+            function(*arguments)
         for name in ("x", "h", "b"):
-            turn_embedding(name)
+            turn_embedding(name, 0)
+            turn_small_weight(0, name)
 
         unit_columns = const.tile([P, P], F32)
-        vector_bank = psum_turn.tile([P, P], BF16, tag="turned")
+        vector_bank = psum_turn.tile([P, P], BF16, tag="turned", name="turned_vectors")
         nc.tensor.transpose(vector_bank[:], vector_rows[:], ident_bf16[:])
         nc.scalar.copy(out=unit_columns[:], in_=vector_bank[:])
 
-        c_sb = keep.tile([P, BATCH_TILES, H], BF16)
-        cell_i = keep.tile([P, UNIT_BLOCKS, B], F32)
-        cell_f = keep.tile([P, UNIT_BLOCKS, B], F32)
-        free_axis_vectors = {}
+        gate_banks = [(pair, position, k) for pair in range(PAIRS) for position in range(GATES - 1) for k in range(GATE_BANKS)]
+        for t in range(quantise_slot(STEPS_PER_HALF_GATE) - TURN_LEAD - LOAD_LEAD, LAST_SLOT + 1):
+            is_tile, z_tile = 0 <= t < N_TILES, 0 <= t + 2 < N_TILES
+            turned = [q for q in range(STEPS_PER_HALF_GATE, N_STEPS) if quantise_slot(q) == t + TURN_LEAD]
+            quantised = [q for q in range(STEPS_PER_HALF_GATE, N_STEPS) if quantise_slot(q) == t]
+            products = [b for b in gate_banks if bank_slot(*b) == t - 1]
 
-        tiles, rows, cell_state = {}, {}, {}
-        for t in range(STEPS_PER_HALF_GATE - (TURN_AHEAD + LOAD_AHEAD), N_TILES + LAST_LAG):
-            has_tile = 0 <= t < N_TILES
-            row0, row1, row2 = [completed_row(t - lag) for lag in range(LAST_LAG + 1)]
-
-            if has_tile:
-                read_psum(t, tiles[t])
-            if row1 is not None and GATE_ORDER[row1[0]] == GATE_O:
-                row = rows[row1]
-                centre_and_gain(row["pre"][:], row["pre"][:], row["neg_mean"], free_axis_vectors["gain_o"][:])
-            if 0 <= t + 1 < N_TILES:
-                tiles[t + 1] = start_tile(t + 1)
-
-            q = t + TURN_AHEAD + LOAD_AHEAD
-            if STEPS_PER_HALF_GATE <= q < N_STEPS and q % PASSES == 0:
-                load_step(q)
-            q = t + TURN_AHEAD
-            if STEPS_PER_HALF_GATE <= q < N_STEPS:
-                turn_step(q, t < VECTOR_HELPS_UNTIL)
-
-            if has_tile and t // TILES_PER_GATE + 1 < GATES:
-                next_position, slot_in_gate = t // TILES_PER_GATE + 1, t % TILES_PER_GATE
-                if slot_in_gate == 0:
+            for q in range(STEPS_PER_HALF_GATE, N_STEPS, PASSES):
+                if quantise_slot(q) == t + TURN_LEAD + LOAD_LEAD:
+                    load_step(q)
+            for position in range(1, GATES):
+                if t == position * TILES_PER_GATE - 7:
                     for name in ("x", "h", "b"):
-                        load_small_weight(next_position, name, gate_parts[next_position])
-                if slot_in_gate in (1, 2, 3):
-                    turn_small_weight(("x", "h", "b")[slot_in_gate - 1], gate_parts[next_position])
-            if t == 0:
-                nc.sync.dma_start(out=c_sb[:], in_=c.rearrange("(m p) n -> p m n", p=P))
-            if t == BROADCAST_SLOT:
-                for name, vector in (
-                    ("gain_c", lnc_gamma), ("shift_c", lnc_beta),
-                    ("gain_o", ln_gamma[GATE_O, :]), ("shift_o", ln_beta[GATE_O, :]),
-                ):
-                    free_axis_vectors[name] = keep.tile([P, H], BF16, name=name)
-                    nc.gpsimd.dma_start(out=free_axis_vectors[name][:], in_=vector.partition_broadcast(P))
-
-            if has_tile:
-                add_products(tiles[t])
-            q = t + QUANTISE_AHEAD
-            if STEPS_PER_HALF_GATE <= q < N_STEPS:
-                quantise_step(q)
-            if has_tile:
-                finish_tile(t, tiles[t])
-            if 0 <= t + 1 < N_TILES:
-                start_offset(t + 1, tiles[t + 1])
-
-            if row0 is not None:
-                row = rows[row0]
-                row["neg_mean"], row["inv_std"] = start_stats(row["pre"][:], row["sums"])
-            if row1 is not None:
-                row = rows[row1]
-                if GATE_ORDER[row1[0]] == GATE_O:
-                    scale_and_shift(row["pre"][:], row["inv_std"], free_axis_vectors["shift_o"][:])
-                    nc.scalar.activation(out=row["pre"][:], in_=row["pre"][:], func=ACT.Sigmoid)
-                else:
-                    offset = stats.tile([P, 1], F32)
-                    nc.gpsimd.tensor_tensor(out=offset[:], in0=row["neg_mean"][:], in1=row["inv_std"][:], op=ALU.mult)
-                    nc.scalar.activation(
-                        out=row["pre"][:], in_=row["pre"][:], func=ACT.Identity, scale=row["inv_std"][:, 0:1], bias=offset[:, 0:1],
+                        load_small_weight(position, name)
+            if t == 3:
+                for name in ("x", "h"):
+                    load_act(name, 1)
+            if t == 6:
+                for name in ("x", "h", "b"):
+                    load_embedding(name, 1)
+            for pair in range(PAIRS):
+                if t == pair * TILES_PER_PAIR + 10:
+                    c_rows[pair] = keep.tile([P, PAIR, H], BF16, name="c_rows", tag="c_rows")
+                    nc.sync.dma_start(
+                        out=c_rows[pair][:], in_=c[pair * SAMPLES : (pair + 1) * SAMPLES, :].rearrange("(s p) n -> p s n", p=P),
                     )
+            if t == 10:
+                for name, vector in (
+                    ("gain_o", ln_gamma[GATE_O, :]), ("shift_o", ln_beta[GATE_O, :]), ("gain_c", lnc_gamma), ("shift_c", lnc_beta),
+                ):
+                    unit_vectors[name] = keep.tile([P, H], BF16, name=name)
+                    nc.gpsimd.dma_start(out=unit_vectors[name][:], in_=vector.partition_broadcast(P))
 
-            if has_tile and t >= TILES_PER_GATE:
-                previous, slot_in_gate = t // TILES_PER_GATE - 1, t % TILES_PER_GATE
-                if 1 <= slot_in_gate < FIRST_BACK_SLOT:
-                    for j in range((slot_in_gate - 1) * BLOCKS_PER_SLOT, slot_in_gate * BLOCKS_PER_SLOT):
-                        gate_block(previous, j)
-                if GATE_ORDER[previous] == GATE_F:
-                    first = (slot_in_gate - FIRST_BACK_SLOT - 1) * BACK_PER_SLOT
-                    if 0 <= first < BATCH_TILES:
-                        for m in range(first, first + BACK_PER_SLOT):
-                            finish_cell(m, cell_state[m])
-                    first = (slot_in_gate - FIRST_BACK_SLOT) * BACK_PER_SLOT
-                    if 0 <= first < BATCH_TILES:
-                        for m in range(first, first + BACK_PER_SLOT):
-                            cell_state[m] = cell_back(m)
+            if is_tile:
+                multiply(t, "x")
+                multiply(t, "h")
 
-            if row2 is not None and GATE_ORDER[row2[0]] == GATE_O:
-                m = row2[1]
-                new_h = results.tile([P, H], F32, tag="result")
-                nc.vector.tensor_tensor(out=new_h[:], in0=rows[row2]["pre"][:], in1=cell_state[m]["values"][:], op=ALU.mult)
-                nc.sync.dma_start(out=out_0[m * P : (m + 1) * P, :], in_=new_h[:])
+            matmuls = []
+            if z_tile:
+                matmuls += [(start_z, (t + 2, "x")), (start_z, (t + 2, "h"))]
+            if is_tile:
+                matmuls += [(start_offset, (t,)), (add_bias, (t,))]
+            copies = [(copy_z, (t + 2, name)) for name in ("x", "h")] if z_tile else []
+            for q in turned:
+                for pair in range(2):
+                    for function, arguments in matmuls[:1]:
+                        function(*arguments)
+                    matmuls = matmuls[1:]
+                    turn_step(q, pair, False)
+                    for function, arguments in copies[:1]:
+                        function(*arguments)
+                    copies = copies[1:]
+            for function, arguments in matmuls + copies:
+                function(*arguments)
+            for b in products[:1]:
+                gate_product(*b)
+            for q in quantised[:1]:
+                quantise_step(q)
+            for b in products[1:]:
+                gate_product(*b)
+            for b in gate_banks:
+                if bank_slot(*b) == t:
+                    gate_bank(*b)
+            for position in range(1, GATES):
+                if 0 <= t - (position * TILES_PER_GATE - 5) < 3:
+                    turn_small_weight(position, ("x", "h", "b")[t - (position * TILES_PER_GATE - 5)])
+            if t in (6, 7):
+                for g in range(PASSES):
+                    waiting_act = turn_act(("x", "h")[t - 6], g, False)
+                    quantise_act(("x", "h")[t - 6], 1, g, waiting_act)
+            if t in (9, 10, 11):
+                turn_embedding(("x", "h", "b")[t - 9], 1)
+            for m in range(BATCH_TILES):
+                if t == back_slot(m):
+                    cell_back(m)
+            if 0 <= t + 1 < N_TILES:
+                start_products(t + 1)
+
+            if is_tile:
+                add_products(t)
+            for q in quantised[1:]:
+                quantise_step(q)
+
+            done, before = completed_row(t - 1), completed_row(t - 2)
+            if before is not None:
+                if GATE_ORDER[before[0]] == GATE_O:
+                    apply_norm(rows[before]["values"][:], rows[before], "gain_o", "shift_o")
+                    nc.scalar.activation(out=rows[before]["values"][:], in_=rows[before]["values"][:], func=ACT.Sigmoid)
+                else:
+                    normalise(rows[before])
+            if is_tile:
+                finish_tile(t)
+            if done is not None:
+                start_stats(rows[done])
+            for m in range(BATCH_TILES):
+                if t == back_slot(m) + 2:
+                    finish_cell(m)
+                if t == back_slot(m) + 1:
+                    start_stats(cells[m])
+            for m in range(BATCH_TILES):
+                if t == new_h_slot(m):
+                    finish_h(m)

@@ -19,17 +19,16 @@ H = 1024
 E = 128
 GATES = 4
 BATCH_TILES = B // P
-PAIR = 2
-PAIRS = BATCH_TILES // PAIR
-SAMPLES = PAIR * P
+GROUPS = ((0, 1), (2,), (3,))
 K_PASS = 4 * P
 PASSES = K // K_PASS
 ROWS = 512
 HALVES = H // ROWS
 UNIT_BLOCKS = H // P
-TILES_PER_GATE = HALVES * PAIR
-TILES_PER_PAIR = GATES * TILES_PER_GATE
-N_TILES = PAIRS * TILES_PER_PAIR
+TILES = [
+    (position, half, m) for group in GROUPS for position in range(GATES) for half in range(HALVES) for m in group
+]
+N_TILES = len(TILES)
 EPS = 1e-6
 
 GATE_I, GATE_F, GATE_G, GATE_O = 0, 1, 2, 3
@@ -39,58 +38,50 @@ STEPS_PER_HALF_GATE = 2 * PASSES
 HALF_GATES = GATES * HALVES
 N_STEPS = HALF_GATES * STEPS_PER_HALF_GATE
 SCALE_ROWS = 4
-STEPS_PER_SLOT = STEPS_PER_HALF_GATE // PAIR
+STEPS_PER_SLOT = STEPS_PER_HALF_GATE // len(GROUPS[0])
 TURN_LEAD = 1
 LOAD_LEAD = 1
 
 BIAS_COLUMN = 2 * GATES * UNIT_BLOCKS
 FIRST_BIAS_ROW_GATE = 1
-GATE_BANKS = UNIT_BLOCKS // 2
+BANK_COLUMNS = 512
 BANKS_PER_SLOT = 2
 
 FLOPS = 2 * (2 * B * K * GATES * H) + 3 * (2 * B * E * GATES * H)
 
 
-def where(t):
-    pair, rest = divmod(t, TILES_PER_PAIR)
-    position, place = divmod(rest, TILES_PER_GATE)
-    if pair == 0:
-        half, i = divmod(place, PAIR)
-    else:
-        i, half = divmod(place, HALVES)
-    return position, half, pair * PAIR + i
+def row_slot(position, m):
+    return TILES.index((position, HALVES - 1, m))
 
 
 def scale_row(name, g):
     return SCALE_ROWS * (PASSES * ("x", "h").index(name) + g)
 
 
-def completed_row(t):
-    if 0 <= t < N_TILES and where(t)[1] == HALVES - 1:
-        return where(t)[0], where(t)[2]
-    return None
-
-
 def quantise_slot(q):
     return q // STEPS_PER_SLOT - 3
 
 
-def bank_slot(pair, position, k):
-    return pair * TILES_PER_PAIR + (position + 1) * TILES_PER_GATE + 2 + k // BANKS_PER_SLOT
+def blocks_per_bank(group):
+    return BANK_COLUMNS // (P * len(group))
+
+
+def norm_slot(position, m):
+    return row_slot(position, m) + 2
+
+
+def bank_slot(group, position, k):
+    return norm_slot(position, group[-1]) + 1 + k // BANKS_PER_SLOT
 
 
 def back_slot(m):
-    pair, i = divmod(m, PAIR)
-    last = bank_slot(pair, GATE_ORDER.index(GATE_F), GATE_BANKS - 1)
-    return last + 2 + (i if pair < PAIRS - 1 else 0)
-
-
-def row_slot(position, m):
-    return [t for t in range(N_TILES) if completed_row(t) == (position, m)][0]
+    group = [group for group in GROUPS if m in group][0]
+    last_bank = UNIT_BLOCKS // blocks_per_bank(group) - 1
+    return bank_slot(group, GATE_ORDER.index(GATE_F), last_bank) + 2 + group.index(m)
 
 
 def new_h_slot(m):
-    return max(back_slot(m), row_slot(GATES - 1, m)) + 3
+    return max(back_slot(m) + 3, norm_slot(GATES - 1, m) + 1) + 1
 
 
 LAST_SLOT = new_h_slot(BATCH_TILES - 1)
@@ -117,9 +108,10 @@ def tile_hyperlstmcell_pb_kernel(
         pre_pool = ctx.enter_context(tc.tile_pool(name="pre", bufs=5))
         sums_pool = ctx.enter_context(tc.tile_pool(name="sums", bufs=8))
         block_pool = ctx.enter_context(tc.tile_pool(name="block", bufs=2))
-        cell_rows = ctx.enter_context(tc.tile_pool(name="cell_rows", bufs=PAIR))
+        cell_rows = ctx.enter_context(tc.tile_pool(name="cell_rows", bufs=2))
         results = ctx.enter_context(tc.tile_pool(name="results", bufs=1))
         scratch = ctx.enter_context(tc.tile_pool(name="scratch", bufs=1))
+        c_pool = ctx.enter_context(tc.tile_pool(name="c_rows", bufs=2))
         stats = ctx.enter_context(tc.tile_pool(name="stats", bufs=8))
         psum_out = ctx.enter_context(tc.psum_pool(name="psum_out", bufs=1))
         psum_turn = ctx.enter_context(tc.psum_pool(name="psum_turn", bufs=3))
@@ -137,18 +129,18 @@ def tile_hyperlstmcell_pb_kernel(
         act_rows, emb_rows, c_rows, emb_t, small_t, unit_vectors = {}, {}, {}, {}, {}, {}
         codes, scales = {}, {}
 
-        def load_act(name, pair):
-            act_rows[name] = pre_pool.tile([P, PAIR, K], BF16, name="act_rows_" + name, tag="pre")
+        def load_act(name, first):
+            if first == 0:
+                act_rows[name] = pre_pool.tile([P, 2, K], BF16, name="act_rows_" + name, tag="pre")[:]
             nc.sync.dma_start(
-                out=act_rows[name][:],
-                in_=activation[name][pair * SAMPLES : (pair + 1) * SAMPLES, :].rearrange("(r p) k -> p r k", p=P),
+                out=act_rows[name], in_=activation[name][first : first + 2 * P, :].rearrange("(r p) k -> p r k", p=P),
             )
 
-        def load_embedding(name, pair):
-            emb_rows[name] = pre_pool.tile([P, PAIR, GATES * E], BF16, name="emb_rows_" + name, tag="pre")
+        def load_embedding(name, first):
+            if first == 0:
+                emb_rows[name] = pre_pool.tile([P, 2, GATES * E], BF16, name="emb_rows_" + name, tag="pre")[:]
             nc.sync.dma_start(
-                out=emb_rows[name][:],
-                in_=embedding[name][pair * SAMPLES : (pair + 1) * SAMPLES].rearrange("(m p) g e -> p m (g e)", p=P),
+                out=emb_rows[name], in_=embedding[name][first : first + 2 * P].rearrange("(m p) g e -> p m (g e)", p=P),
             )
 
         def load_step(q):
@@ -186,12 +178,12 @@ def tile_hyperlstmcell_pb_kernel(
         scales["act"] = keep.tile([P, B], U8, align_bytes=64, name="act_scales")
 
         def turn_act(name, g, on_vector):
-            grouped = grouped_pool.tile([P, 4 * SAMPLES], BF16, align_bytes=64, name="act_grouped", tag="grouped")
+            grouped = grouped_pool.tile([P, 8 * P], BF16, align_bytes=64, name="act_grouped", tag="grouped")
             turn_rows(act_rows[name], 0, g, grouped, 0, on_vector)
             return grouped
 
-        def quantise_act(name, pair, g, grouped):
-            samples = slice(pair * SAMPLES, (pair + 1) * SAMPLES)
+        def quantise_act(name, first, g, grouped):
+            samples = slice(first, first + 2 * P)
             nc.vector.quantize_mx(
                 out=codes["act", name][:, g, samples].bitcast(FP8X4), scales=scales["act"][scale_row(name, g) : P, samples],
                 in_=grouped[:],
@@ -223,10 +215,10 @@ def tile_hyperlstmcell_pb_kernel(
         for name in ("x", "h", "b"):
             emb_t[name] = keep.tile([P, GATES, B], BF16, name="emb_t_" + name)
 
-        def turn_embedding(name, pair):
+        def turn_embedding(name, first):
             transpose_eight(
-                [emb_rows[name][:, i, gate * E : (gate + 1) * E] for gate in range(GATES) for i in range(PAIR)],
-                emb_t[name][:, :, pair * SAMPLES : (pair + 1) * SAMPLES], g=GATES,
+                [emb_rows[name][:, i, gate * E : (gate + 1) * E] for gate in range(GATES) for i in range(2)],
+                emb_t[name][:, :, first : first + 2 * P], g=GATES,
             )
 
         def turn_small_weight(position, name):
@@ -235,7 +227,7 @@ def tile_hyperlstmcell_pb_kernel(
             transpose_eight([rows_sb[:, j, :] for j in range(UNIT_BLOCKS)], small_t[position, name][:])
 
         def start_z(t, name):
-            position, half, m = where(t)
+            position, half, m = TILES[t]
             z = tiles.setdefault(t, {})["z_" + name] = psum_out.tile([P, ROWS], F32, name="z_" + name)
             nc.tensor.matmul(
                 out=z[:], lhsT=emb_t[name][:, GATE_ORDER[position], m * P : (m + 1) * P],
@@ -248,7 +240,7 @@ def tile_hyperlstmcell_pb_kernel(
             nc.scalar.copy(out=tile["z_sb_" + name][:], in_=tile["z_" + name][:])
 
         def start_products(t):
-            position, half, m = where(t)
+            position, half, m = TILES[t]
             samples = slice(m * P, (m + 1) * P)
             half_gate = HALVES * position + half
             for name in ("x", "h"):
@@ -265,7 +257,7 @@ def tile_hyperlstmcell_pb_kernel(
                     )
 
         def start_offset(t):
-            position, half, m = where(t)
+            position, half, m = TILES[t]
             z_b = tiles[t]["z_b"] = psum_out.tile([P, ROWS], F32, name="z_b")
             nc.tensor.matmul(
                 out=z_b[:], lhsT=emb_t["b"][:, GATE_ORDER[position], m * P : (m + 1) * P],
@@ -273,7 +265,7 @@ def tile_hyperlstmcell_pb_kernel(
             )
 
         def add_bias(t):
-            position, half, m = where(t)
+            position, half, m = TILES[t]
             gate, z_b = GATE_ORDER[position], tiles[t]["z_b"]
             if position > 0:
                 first_unit = (gate - FIRST_BIAS_ROW_GATE) * H + half * ROWS
@@ -300,7 +292,7 @@ def tile_hyperlstmcell_pb_kernel(
             nc.vector.tensor_tensor(out=tile["term_x"][:], in0=tile["term_x"][:], in1=tile["term_h"][:], op=ALU.add)
 
         def finish_tile(t):
-            position, half, m = where(t)
+            position, half, m = TILES[t]
             if half == 0:
                 rows[position, m] = {
                     "values": pre_pool.tile([P, H], F32, name="pre"), "sums": sums_pool.tile([P, HALVES], F32, name="sums"),
@@ -337,44 +329,46 @@ def tile_hyperlstmcell_pb_kernel(
                 op0=ALU.add, op1=ALU.mult,
             )
 
-        def gate_bank(pair, position, k):
-            gate = GATE_ORDER[position]
-            bank = psum_turn.tile([P, 2, SAMPLES], F32, tag="turned", name="turned_gate")
-            for i in range(2):
-                for s in range(PAIR):
+        def bank_blocks(group, k):
+            return range(k * blocks_per_bank(group), (k + 1) * blocks_per_bank(group))
+
+        def gate_bank(group, position, k):
+            gate, blocks, samples = GATE_ORDER[position], bank_blocks(group, k), P * len(group)
+            bank = psum_turn.tile([P, len(blocks), samples], F32, tag="turned", name="turned_gate")
+            for i, j in enumerate(blocks):
+                for s, m in enumerate(group):
                     nc.tensor.transpose(
-                        bank[:, i, s * P : (s + 1) * P],
-                        rows[position, PAIR * pair + s]["values"][:, (2 * k + i) * P : (2 * k + i + 1) * P], ident_f32[:],
+                        bank[:, i, s * P : (s + 1) * P], rows[position, m]["values"][:, j * P : (j + 1) * P], ident_f32[:],
                     )
             if gate == GATE_I:
-                target = cell_i[:, 2 * k : 2 * k + 2, :]
+                target = cell_i[:, blocks[0] : blocks[-1] + 1, :samples]
             else:
-                activated[position, k] = block_pool.tile([P, 2, SAMPLES], F32, name="activated")
+                activated[position, k] = block_pool.tile([P, len(blocks), samples], F32, name="activated")
                 target = activated[position, k][:]
-            for i in range(2):
-                column = gate * UNIT_BLOCKS + 2 * k + i
+            for i, j in enumerate(blocks):
+                column = gate * UNIT_BLOCKS + j
                 nc.scalar.activation(
                     out=target[:, i, :], in_=bank[:, i, :], func=ACT.Tanh if gate == GATE_G else ACT.Sigmoid,
                     scale=unit_columns[:, column : column + 1],
                     bias=unit_columns[:, GATES * UNIT_BLOCKS + column : GATES * UNIT_BLOCKS + column + 1],
                 )
 
-        def gate_product(pair, position, k):
-            gate = GATE_ORDER[position]
-            blocks = slice(2 * k, 2 * k + 2)
+        def gate_product(group, position, k):
+            gate, blocks, samples = GATE_ORDER[position], bank_blocks(group, k), P * len(group)
+            term = (cell_f if gate == GATE_F else cell_i)[:, blocks[0] : blocks[-1] + 1, :samples]
             if gate == GATE_G:
-                nc.vector.tensor_tensor(
-                    out=cell_i[:, blocks, :], in0=cell_i[:, blocks, :], in1=activated[position, k][:], op=ALU.mult,
-                )
+                nc.vector.tensor_tensor(out=term, in0=term, in1=activated[position, k][:], op=ALU.mult)
             if gate == GATE_F:
-                c_bank = psum_turn.tile([P, 2, SAMPLES], BF16, tag="turned", name="turned_c")
-                for i in range(2):
-                    for s in range(PAIR):
+                c_bank = psum_turn.tile([P, len(blocks), samples], BF16, tag="turned", name="turned_c")
+                for i, j in enumerate(blocks):
+                    for s, m in enumerate(group):
                         nc.tensor.transpose(
-                            c_bank[:, i, s * P : (s + 1) * P], c_rows[pair][:, s, (2 * k + i) * P : (2 * k + i + 1) * P],
-                            ident_bf16[:],
+                            c_bank[:, i, s * P : (s + 1) * P], c_rows[m][:, j * P : (j + 1) * P], ident_bf16[:],
                         )
-                nc.vector.tensor_tensor(out=cell_f[:, blocks, :], in0=c_bank[:], in1=activated[position, k][:], op=ALU.mult)
+                nc.vector.tensor_tensor(out=term, in0=c_bank[:], in1=activated[position, k][:], op=ALU.mult)
+
+        def sample_slot(m):
+            return [group.index(m) for group in GROUPS if m in group][0]
 
         def cell_back(m):
             row = cells[m] = {
@@ -386,7 +380,7 @@ def tile_hyperlstmcell_pb_kernel(
                     for term in (cell_i, cell_f):
                         nc.tensor.matmul(
                             out=bank[:, i * P : (i + 1) * P],
-                            lhsT=term[:, half * (ROWS // P) + i, m % PAIR * P : (m % PAIR + 1) * P],
+                            lhsT=term[:, half * (ROWS // P) + i, sample_slot(m) * P : (sample_slot(m) + 1) * P],
                             rhs=ident_f32[:], is_transpose=True, start=(term is cell_i), stop=(term is cell_f),
                         )
                 nc.scalar.activation(
@@ -394,20 +388,22 @@ def tile_hyperlstmcell_pb_kernel(
                     accum_out=row["sums"][:, half : half + 1],
                 )
 
-        def apply_norm(out, row, gain, shift):
+        def centre(row, gain):
             nc.vector.scalar_tensor_tensor(
-                out=out, in0=row["values"][:], scalar=row["neg_mean"][:, 0:1], in1=unit_vectors[gain][:],
+                out=row["values"][:], in0=row["values"][:], scalar=row["neg_mean"][:, 0:1], in1=unit_vectors[gain][:],
                 op0=ALU.add, op1=ALU.mult,
             )
+
+        def shift(out, row, vector):
             nc.vector.scalar_tensor_tensor(
-                out=out, in0=out, scalar=row["inv_std"][:, 0:1], in1=unit_vectors[shift][:], op0=ALU.mult, op1=ALU.add,
+                out=out, in0=row["values"][:], scalar=row["inv_std"][:, 0:1], in1=unit_vectors[vector][:],
+                op0=ALU.mult, op1=ALU.add,
             )
 
-        def finish_cell(m):
-            new_c = results.tile([P, H], F32, name="new_c")
-            apply_norm(new_c[:], cells[m], "gain_c", "shift_c")
+        def shift_cell(m):
+            new_c = cells[m]["new_c"] = results.tile([P, H], F32, name="new_c")
+            shift(new_c[:], cells[m], "shift_c")
             nc.sync.dma_start(out=out_1[m * P : (m + 1) * P, :], in_=new_c[:])
-            nc.scalar.activation(out=cells[m]["values"][:], in_=new_c[:], func=ACT.Tanh)
 
         def finish_h(m):
             values = cells[m]["values"]
@@ -415,9 +411,11 @@ def tile_hyperlstmcell_pb_kernel(
             nc.sync.dma_start(out=out_0[m * P : (m + 1) * P, :], in_=values[:])
 
 
+        ctx.enter_context(tc.manual_schedule())
+
         activated = {}
-        cell_i = keep.tile([P, UNIT_BLOCKS, SAMPLES], F32)
-        cell_f = keep.tile([P, UNIT_BLOCKS, SAMPLES], F32)
+        cell_i = keep.tile([P, UNIT_BLOCKS, 2 * P], F32)
+        cell_f = keep.tile([P, UNIT_BLOCKS, 2 * P], F32)
         for i, name in enumerate(("x", "h")):
             load_act(name, 0)
             load_step(PASSES * i)
@@ -446,11 +444,14 @@ def tile_hyperlstmcell_pb_kernel(
             for g in range(PASSES):
                 grouped = turn_act(name, g, g == 1)
                 waiting.append((quantise_act, (name, 0, g, grouped)))
+                if len(waiting) > 1:
+                    function, arguments = waiting.pop(0)
+                    function(*arguments)
             for q in range(PASSES * i, PASSES * (i + 1)):
                 for pair in range(2):
                     turn_step(q, pair, pair == 1)
                 waiting.append((quantise_step, (q,)))
-                while len(waiting) > 1:
+                if len(waiting) > 1:
                     function, arguments = waiting.pop(0)
                     function(*arguments)
         for function, arguments in waiting:
@@ -464,7 +465,12 @@ def tile_hyperlstmcell_pb_kernel(
         nc.tensor.transpose(vector_bank[:], vector_rows[:], ident_bf16[:])
         nc.scalar.copy(out=unit_columns[:], in_=vector_bank[:])
 
-        gate_banks = [(pair, position, k) for pair in range(PAIRS) for position in range(GATES - 1) for k in range(GATE_BANKS)]
+        act_waiting = []
+        gate_banks = [
+            (group, position, k)
+            for group in GROUPS for position in range(GATES - 1) for k in range(UNIT_BLOCKS // blocks_per_bank(group))
+        ]
+        all_rows = [(position, m) for position in range(GATES) for m in range(BATCH_TILES)]
         for t in range(quantise_slot(STEPS_PER_HALF_GATE) - TURN_LEAD - LOAD_LEAD, LAST_SLOT + 1):
             is_tile, z_tile = 0 <= t < N_TILES, 0 <= t + 2 < N_TILES
             turned = [q for q in range(STEPS_PER_HALF_GATE, N_STEPS) if quantise_slot(q) == t + TURN_LEAD]
@@ -475,21 +481,23 @@ def tile_hyperlstmcell_pb_kernel(
                 if quantise_slot(q) == t + TURN_LEAD + LOAD_LEAD:
                     load_step(q)
             for position in range(1, GATES):
-                if t == position * TILES_PER_GATE - 7:
+                if t == 4 * position - 6:
                     for name in ("x", "h", "b"):
                         load_small_weight(position, name)
-            if t == 3:
-                for name in ("x", "h"):
-                    load_act(name, 1)
-            if t == 6:
-                for name in ("x", "h", "b"):
-                    load_embedding(name, 1)
-            for pair in range(PAIRS):
-                if t == pair * TILES_PER_PAIR + 10:
-                    c_rows[pair] = keep.tile([P, PAIR, H], BF16, name="c_rows", tag="c_rows")
-                    nc.sync.dma_start(
-                        out=c_rows[pair][:], in_=c[pair * SAMPLES : (pair + 1) * SAMPLES, :].rearrange("(s p) n -> p s n", p=P),
-                    )
+            if t == 11:
+                shared = big_rows.tile([P, 4, K], BF16, name="big")
+                for i, name in enumerate(("x", "h", "b")):
+                    emb_rows[name] = shared[:, i, :].rearrange("p (m g) -> p m g", m=2)
+                    load_embedding(name, 2 * P)
+            if t == 12:
+                shared = big_rows.tile([P, 4, K], BF16, name="big")
+                for i, name in enumerate(("x", "h")):
+                    act_rows[name] = shared[:, 2 * i : 2 * i + 2, :]
+                    load_act(name, 2 * P)
+            for m in range(BATCH_TILES):
+                if t == row_slot(GATE_ORDER.index(GATE_F), m) - 2:
+                    c_rows[m] = c_pool.tile([P, H], BF16, name="c_rows")
+                    nc.sync.dma_start(out=c_rows[m][:], in_=c[m * P : (m + 1) * P, :])
             if t == 10:
                 for name, vector in (
                     ("gain_o", ln_gamma[GATE_O, :]), ("shift_o", ln_beta[GATE_O, :]), ("gain_c", lnc_gamma), ("shift_c", lnc_beta),
@@ -497,9 +505,19 @@ def tile_hyperlstmcell_pb_kernel(
                     unit_vectors[name] = keep.tile([P, H], BF16, name=name)
                     nc.gpsimd.dma_start(out=unit_vectors[name][:], in_=vector.partition_broadcast(P))
 
+            done_rows = [rows[row] for row in all_rows if row_slot(*row) == t - 1]
+            done_rows += [cells[m] for m in range(BATCH_TILES) if t == back_slot(m) + 1]
             if is_tile:
                 multiply(t, "x")
                 multiply(t, "h")
+            for q in quantised:
+                quantise_step(q)
+            for name, g, grouped in act_waiting:
+                quantise_act(name, 2 * P, g, grouped)
+            act_waiting = []
+
+            for b in products:
+                gate_product(*b)
 
             matmuls = []
             if z_tile:
@@ -507,62 +525,54 @@ def tile_hyperlstmcell_pb_kernel(
             if is_tile:
                 matmuls += [(start_offset, (t,)), (add_bias, (t,))]
             copies = [(copy_z, (t + 2, name)) for name in ("x", "h")] if z_tile else []
-            for q in turned:
-                for pair in range(2):
-                    for function, arguments in matmuls[:1]:
-                        function(*arguments)
-                    matmuls = matmuls[1:]
-                    turn_step(q, pair, False)
-                    for function, arguments in copies[:1]:
-                        function(*arguments)
-                    copies = copies[1:]
-            for function, arguments in matmuls + copies:
-                function(*arguments)
-            for b in products[:1]:
-                gate_product(*b)
-            for q in quantised[:1]:
-                quantise_step(q)
-            for b in products[1:]:
-                gate_product(*b)
-            for b in gate_banks:
-                if bank_slot(*b) == t:
-                    gate_bank(*b)
+            transposes = [(turn_step, (q, pair, False)) for q in turned for pair in range(2)]
+            transposes += [(gate_bank, b) for b in gate_banks if bank_slot(*b) == t]
             for position in range(1, GATES):
-                if 0 <= t - (position * TILES_PER_GATE - 5) < 3:
-                    turn_small_weight(position, ("x", "h", "b")[t - (position * TILES_PER_GATE - 5)])
-            if t in (6, 7):
-                for g in range(PASSES):
-                    waiting_act = turn_act(("x", "h")[t - 6], g, False)
-                    quantise_act(("x", "h")[t - 6], 1, g, waiting_act)
-            if t in (9, 10, 11):
-                turn_embedding(("x", "h", "b")[t - 9], 1)
+                if 0 <= t - (4 * position - 5) < 3:
+                    transposes.append((turn_small_weight, (position, ("x", "h", "b")[t - (4 * position - 5)])))
+            if t in (12, 13):
+                transposes += [(turn_embedding, (name, 2 * P)) for name in (("x", "h") if t == 12 else ("b",))]
+            while matmuls or transposes or copies:
+                for work_list in (matmuls, transposes, copies):
+                    for function, arguments in work_list[:1]:
+                        function(*arguments)
+                matmuls, transposes, copies = matmuls[1:], transposes[1:], copies[1:]
+            if t in (13, 14):
+                name = ("x", "h")[t - 13]
+                act_waiting = [(name, g, turn_act(name, g, False)) for g in range(PASSES)]
             for m in range(BATCH_TILES):
                 if t == back_slot(m):
                     cell_back(m)
             if 0 <= t + 1 < N_TILES:
                 start_products(t + 1)
 
+            for m in range(BATCH_TILES):
+                if t == back_slot(m) + 3:
+                    nc.scalar.activation(out=cells[m]["values"][:], in_=cells[m]["new_c"][:], func=ACT.Tanh)
+                if t == norm_slot(GATES - 1, m) + 1:
+                    values = rows[GATES - 1, m]["values"]
+                    nc.scalar.activation(out=values[:], in_=values[:], func=ACT.Sigmoid)
+            for row in done_rows:
+                start_stats(row)
+
             if is_tile:
                 add_products(t)
-            for q in quantised[1:]:
-                quantise_step(q)
-
-            done, before = completed_row(t - 1), completed_row(t - 2)
-            if before is not None:
-                if GATE_ORDER[before[0]] == GATE_O:
-                    apply_norm(rows[before]["values"][:], rows[before], "gain_o", "shift_o")
-                    nc.scalar.activation(out=rows[before]["values"][:], in_=rows[before]["values"][:], func=ACT.Sigmoid)
-                else:
-                    normalise(rows[before])
-            if is_tile:
-                finish_tile(t)
-            if done is not None:
-                start_stats(rows[done])
+            normed = []
+            for row in all_rows:
+                if t == norm_slot(*row):
+                    if GATE_ORDER[row[0]] == GATE_O:
+                        centre(rows[row], "gain_o")
+                        normed.append((shift, (rows[row]["values"][:], rows[row], "shift_o")))
+                    else:
+                        normalise(rows[row])
             for m in range(BATCH_TILES):
                 if t == back_slot(m) + 2:
-                    finish_cell(m)
-                if t == back_slot(m) + 1:
-                    start_stats(cells[m])
+                    centre(cells[m], "gain_c")
+                    normed.append((shift_cell, (m,)))
+            if is_tile:
+                finish_tile(t)
+            for function, arguments in normed:
+                function(*arguments)
             for m in range(BATCH_TILES):
                 if t == new_h_slot(m):
                     finish_h(m)

@@ -25,14 +25,19 @@ PASSES = K // K_PASS
 ROWS = 512
 HALVES = H // ROWS
 UNIT_BLOCKS = H // P
-TILES = [
-    (position, half, m) for group in GROUPS for position in range(GATES) for half in range(HALVES) for m in group
-]
-N_TILES = len(TILES)
 EPS = 1e-6
 
 GATE_I, GATE_F, GATE_G, GATE_O = 0, 1, 2, 3
 GATE_ORDER = (GATE_I, GATE_G, GATE_F, GATE_O)
+TILES = [
+    (position, half, m)
+    for group, positions in (
+        (GROUPS[0], range(GATES)), (GROUPS[1], range(GATES - 1)), (GROUPS[2], range(GATES - 1)),
+        (GROUPS[1], (GATES - 1,)), (GROUPS[2], (GATES - 1,)),
+    )
+    for position in positions for half in range(HALVES) for m in group
+]
+N_TILES = len(TILES)
 
 STEPS_PER_HALF_GATE = 2 * PASSES
 HALF_GATES = GATES * HALVES
@@ -42,10 +47,10 @@ STEPS_PER_SLOT = STEPS_PER_HALF_GATE // len(GROUPS[0])
 TURN_LEAD = 1
 LOAD_LEAD = 1
 
-BIAS_COLUMN = 2 * GATES * UNIT_BLOCKS
-FIRST_BIAS_ROW_GATE = 1
+VECTOR_BIAS_TILES = N_STEPS // STEPS_PER_SLOT - 4
 BANK_COLUMNS = 512
-BANKS_PER_SLOT = 2
+BANKS_PER_SLOT = 1
+BACK_SPACING = 3
 
 FLOPS = 2 * (2 * B * K * GATES * H) + 3 * (2 * B * E * GATES * H)
 
@@ -77,7 +82,7 @@ def bank_slot(group, position, k):
 def back_slot(m):
     group = [group for group in GROUPS if m in group][0]
     last_bank = UNIT_BLOCKS // blocks_per_bank(group) - 1
-    return bank_slot(group, GATE_ORDER.index(GATE_F), last_bank) + 2 + group.index(m)
+    return bank_slot(group, GATE_ORDER.index(GATE_F), last_bank) + 2 + BACK_SPACING * group.index(m)
 
 
 def new_h_slot(m):
@@ -105,11 +110,10 @@ def tile_hyperlstmcell_pb_kernel(
         grouped_pool = ctx.enter_context(tc.tile_pool(name="grouped", bufs=3))
         work = ctx.enter_context(tc.tile_pool(name="work", bufs=2))
         z_pool = ctx.enter_context(tc.tile_pool(name="z_sb", bufs=2))
-        pre_pool = ctx.enter_context(tc.tile_pool(name="pre", bufs=5))
-        sums_pool = ctx.enter_context(tc.tile_pool(name="sums", bufs=8))
+        pre_pool = ctx.enter_context(tc.tile_pool(name="pre", bufs=6))
+        sums_pool = ctx.enter_context(tc.tile_pool(name="sums", bufs=6))
         block_pool = ctx.enter_context(tc.tile_pool(name="block", bufs=2))
         cell_rows = ctx.enter_context(tc.tile_pool(name="cell_rows", bufs=2))
-        results = ctx.enter_context(tc.tile_pool(name="results", bufs=1))
         scratch = ctx.enter_context(tc.tile_pool(name="scratch", bufs=1))
         c_pool = ctx.enter_context(tc.tile_pool(name="c_rows", bufs=2))
         stats = ctx.enter_context(tc.tile_pool(name="stats", bufs=8))
@@ -239,46 +243,45 @@ def tile_hyperlstmcell_pb_kernel(
             tile["z_sb_" + name] = z_pool.tile([P, ROWS], F32, name="z_sb_" + name)
             nc.scalar.copy(out=tile["z_sb_" + name][:], in_=tile["z_" + name][:])
 
-        def start_products(t):
+        def start_product(t, name):
             position, half, m = TILES[t]
             samples = slice(m * P, (m + 1) * P)
             half_gate = HALVES * position + half
-            for name in ("x", "h"):
-                product = tiles[t]["product_" + name] = psum_out.tile([P, ROWS], F32, name="product_" + name)
-                for g in range(PASSES):
-                    nc.tensor.matmul_mx(
-                        out=product[:],
-                        lhsT=codes["act", name][:, g, samples].bitcast(FP8X4),
-                        lhsT_scale=scales["act"][scale_row(name, g) : P, samples],
-                        rhs=codes[half_gate, name][:, g, :].bitcast(FP8X4),
-                        rhs_scale=scales[half_gate][scale_row(name, g) : P, :],
-                        start=(g == 0),
-                        stop=(g == PASSES - 1),
-                    )
+            product = tiles[t]["product_" + name] = psum_out.tile([P, ROWS], F32, name="product_" + name)
+            for g in range(PASSES):
+                nc.tensor.matmul_mx(
+                    out=product[:],
+                    lhsT=codes["act", name][:, g, samples].bitcast(FP8X4),
+                    lhsT_scale=scales["act"][scale_row(name, g) : P, samples],
+                    rhs=codes[half_gate, name][:, g, :].bitcast(FP8X4),
+                    rhs_scale=scales[half_gate][scale_row(name, g) : P, :],
+                    start=(g == 0),
+                    stop=(g == PASSES - 1),
+                )
 
         def start_offset(t):
             position, half, m = TILES[t]
             z_b = tiles[t]["z_b"] = psum_out.tile([P, ROWS], F32, name="z_b")
             nc.tensor.matmul(
                 out=z_b[:], lhsT=emb_t["b"][:, GATE_ORDER[position], m * P : (m + 1) * P],
-                rhs=small_t[position, "b"][:, half * ROWS : (half + 1) * ROWS], start=True, stop=False,
+                rhs=small_t[position, "b"][:, half * ROWS : (half + 1) * ROWS],
+                start=True, stop=(t < VECTOR_BIAS_TILES),
             )
 
         def add_bias(t):
             position, half, m = TILES[t]
-            gate, z_b = GATE_ORDER[position], tiles[t]["z_b"]
-            if position > 0:
-                first_unit = (gate - FIRST_BIAS_ROW_GATE) * H + half * ROWS
-                nc.tensor.matmul(
-                    out=z_b[:], lhsT=ones[:], rhs=bias_rows[:, first_unit : first_unit + ROWS], start=False, stop=True,
-                )
-                return
-            for i in range(ROWS // P):
-                column = BIAS_COLUMN + half * (ROWS // P) + i
-                nc.tensor.matmul(
-                    out=z_b[:, i * P : (i + 1) * P], lhsT=unit_columns[:, column : column + 1].to_broadcast([P, P]),
-                    rhs=ident_f32[:], is_transpose=True, start=False, stop=(i == ROWS // P - 1),
-                )
+            first_unit = GATE_ORDER[position] * H + half * ROWS
+            nc.tensor.matmul(
+                out=tiles[t]["z_b"][:], lhsT=first_row[:], rhs=bias_rows[:, first_unit : first_unit + ROWS],
+                start=False, stop=True,
+            )
+
+        def add_bias_on_vector(t):
+            position, half, m = TILES[t]
+            first_unit, term = GATE_ORDER[position] * H + half * ROWS, tiles[t]["term_x"]
+            nc.vector.tensor_tensor(
+                out=term[:], in0=term[:], in1=bias_rows[:, first_unit : first_unit + ROWS], op=ALU.add,
+            )
 
         def multiply(t, name):
             tile = tiles[t]
@@ -303,31 +306,37 @@ def tile_hyperlstmcell_pb_kernel(
                 in1=tiles[t]["term_x"][:], op0=ALU.mult, op1=ALU.add, accum_out=row["sums"][:, half : half + 1],
             )
 
-        def start_stats(row):
-            neg_mean = row["neg_mean"] = stats.tile([P, 1], F32, name="neg_mean")
-            nc.gpsimd.tensor_scalar(
-                out=neg_mean[:], in0=row["sums"][:, 0:1], scalar1=row["sums"][:, 1:2], scalar2=-1.0 / H,
-                op0=ALU.add, op1=ALU.mult,
-            )
-            squares = scratch.tile([P, H], BF16, name="squares")
-            sum_sq = stats.tile([P, 1], F32, name="sum_sq")
-            nc.scalar.activation(
-                out=squares[:], in_=row["values"][:], func=ACT.Square, bias=neg_mean[:, 0:1], scale=1.0, accum_out=sum_sq[:],
-            )
-            root = stats.tile([P, 1], F32, name="root")
-            nc.gpsimd.tensor_tensor(out=root[:], in0=sum_sq[:], in1=exp_half[:], op=ALU.pow)
-            std_eps = stats.tile([P, 1], F32, name="std_eps")
-            nc.gpsimd.tensor_scalar(
-                out=std_eps[:], in0=root[:], scalar1=1.0 / math.sqrt(H - 1), scalar2=EPS, op0=ALU.mult, op1=ALU.add,
-            )
-            row["inv_std"] = stats.tile([P, 1], F32, name="inv_std")
-            nc.gpsimd.tensor_tensor(out=row["inv_std"][:], in0=std_eps[:], in1=exp_minus_one[:], op=ALU.pow)
+        def start_stats(some_rows):
+            for row in some_rows:
+                numbers = stats.tile([P, 5], F32, name="numbers")
+                row["neg_mean"], row["sum_sq"], row["root"], row["std_eps"], row["inv_std"] = [
+                    numbers[:, i : i + 1] for i in range(5)
+                ]
+                nc.gpsimd.tensor_scalar(
+                    out=row["neg_mean"], in0=row["sums"][:, 0:1], scalar1=row["sums"][:, 1:2], scalar2=-1.0 / H,
+                    op0=ALU.add, op1=ALU.mult,
+                )
+            for row in some_rows:
+                squares = scratch.tile([P, H], BF16, name="squares")
+                nc.scalar.activation(
+                    out=squares[:], in_=row["values"][:], func=ACT.Square, bias=row["neg_mean"], scale=1.0,
+                    accum_out=row["sum_sq"],
+                )
+            for row in some_rows:
+                nc.gpsimd.tensor_tensor(out=row["root"], in0=row["sum_sq"], in1=exp_half[:], op=ALU.pow)
+                nc.gpsimd.tensor_scalar(
+                    out=row["std_eps"], in0=row["root"], scalar1=1.0 / math.sqrt(H - 1), scalar2=EPS, op0=ALU.mult, op1=ALU.add,
+                )
+                nc.gpsimd.tensor_tensor(out=row["inv_std"], in0=row["std_eps"], in1=exp_minus_one[:], op=ALU.pow)
 
         def normalise(row):
             nc.vector.tensor_scalar(
-                out=row["values"][:], in0=row["values"][:], scalar1=row["neg_mean"][:, 0:1], scalar2=row["inv_std"][:, 0:1],
+                out=row["values"][:], in0=row["values"][:], scalar1=row["neg_mean"], scalar2=row["inv_std"],
                 op0=ALU.add, op1=ALU.mult,
             )
+
+        def cell_columns(group):
+            return slice(group[0] % 2 * P, group[0] % 2 * P + P * len(group))
 
         def bank_blocks(group, k):
             return range(k * blocks_per_bank(group), (k + 1) * blocks_per_bank(group))
@@ -341,7 +350,7 @@ def tile_hyperlstmcell_pb_kernel(
                         bank[:, i, s * P : (s + 1) * P], rows[position, m]["values"][:, j * P : (j + 1) * P], ident_f32[:],
                     )
             if gate == GATE_I:
-                target = cell_i[:, blocks[0] : blocks[-1] + 1, :samples]
+                target = cell_i[:, blocks[0] : blocks[-1] + 1, cell_columns(group)]
             else:
                 activated[position, k] = block_pool.tile([P, len(blocks), samples], F32, name="activated")
                 target = activated[position, k][:]
@@ -355,7 +364,7 @@ def tile_hyperlstmcell_pb_kernel(
 
         def gate_product(group, position, k):
             gate, blocks, samples = GATE_ORDER[position], bank_blocks(group, k), P * len(group)
-            term = (cell_f if gate == GATE_F else cell_i)[:, blocks[0] : blocks[-1] + 1, :samples]
+            term = (cell_f if gate == GATE_F else cell_i)[:, blocks[0] : blocks[-1] + 1, cell_columns(group)]
             if gate == GATE_G:
                 nc.vector.tensor_tensor(out=term, in0=term, in1=activated[position, k][:], op=ALU.mult)
             if gate == GATE_F:
@@ -367,9 +376,6 @@ def tile_hyperlstmcell_pb_kernel(
                         )
                 nc.vector.tensor_tensor(out=term, in0=c_bank[:], in1=activated[position, k][:], op=ALU.mult)
 
-        def sample_slot(m):
-            return [group.index(m) for group in GROUPS if m in group][0]
-
         def cell_back(m):
             row = cells[m] = {
                 "values": cell_rows.tile([P, H], F32, name="cell_row"), "sums": sums_pool.tile([P, HALVES], F32, name="cell_sums"),
@@ -380,7 +386,7 @@ def tile_hyperlstmcell_pb_kernel(
                     for term in (cell_i, cell_f):
                         nc.tensor.matmul(
                             out=bank[:, i * P : (i + 1) * P],
-                            lhsT=term[:, half * (ROWS // P) + i, sample_slot(m) * P : (sample_slot(m) + 1) * P],
+                            lhsT=term[:, half * (ROWS // P) + i, m % 2 * P : (m % 2 + 1) * P],
                             rhs=ident_f32[:], is_transpose=True, start=(term is cell_i), stop=(term is cell_f),
                         )
                 nc.scalar.activation(
@@ -390,25 +396,31 @@ def tile_hyperlstmcell_pb_kernel(
 
         def centre(row, gain):
             nc.vector.scalar_tensor_tensor(
-                out=row["values"][:], in0=row["values"][:], scalar=row["neg_mean"][:, 0:1], in1=unit_vectors[gain][:],
+                out=row["values"][:], in0=row["values"][:], scalar=row["neg_mean"], in1=unit_vectors[gain][:],
                 op0=ALU.add, op1=ALU.mult,
             )
 
-        def shift(out, row, vector):
+        def shift(out, row, vector, half):
+            units = slice(half * ROWS, (half + 1) * ROWS)
             nc.vector.scalar_tensor_tensor(
-                out=out, in0=row["values"][:], scalar=row["inv_std"][:, 0:1], in1=unit_vectors[vector][:],
+                out=out[:, units], in0=row["values"][:, units], scalar=row["inv_std"], in1=unit_vectors[vector][:, units],
                 op0=ALU.mult, op1=ALU.add,
             )
 
         def shift_cell(m):
-            new_c = cells[m]["new_c"] = results.tile([P, H], F32, name="new_c")
-            shift(new_c[:], cells[m], "shift_c")
+            new_c = cells[m]["new_c"] = big_rows.tile([P, H], F32, name="new_c", tag="big")
+            for half in range(HALVES):
+                shift(new_c, cells[m], "shift_c", half)
             nc.sync.dma_start(out=out_1[m * P : (m + 1) * P, :], in_=new_c[:])
 
         def finish_h(m):
             values = cells[m]["values"]
-            nc.vector.tensor_tensor(out=values[:], in0=rows[GATES - 1, m]["values"][:], in1=values[:], op=ALU.mult)
-            nc.sync.dma_start(out=out_0[m * P : (m + 1) * P, :], in_=values[:])
+            for half in range(HALVES):
+                units = slice(half * ROWS, (half + 1) * ROWS)
+                nc.vector.tensor_tensor(
+                    out=values[:, units], in0=rows[GATES - 1, m]["values"][:, units], in1=values[:, units], op=ALU.mult,
+                )
+                nc.sync.dma_start(out=out_0[m * P : (m + 1) * P, units], in_=values[:, units])
 
 
         ctx.enter_context(tc.manual_schedule())
@@ -429,15 +441,16 @@ def tile_hyperlstmcell_pb_kernel(
                 out=vector_rows[i * GATES * UNIT_BLOCKS : (i + 1) * GATES * UNIT_BLOCKS, :],
                 in_=vector.rearrange("g (j p) -> (g j) p", p=P),
             )
-        nc.sync.dma_start(
-            out=vector_rows[BIAS_COLUMN : BIAS_COLUMN + UNIT_BLOCKS, :],
-            in_=bias[GATE_ORDER[0] * H : (GATE_ORDER[0] + 1) * H].rearrange("(j p) -> j p", p=P),
-        )
-        ones = const.tile([P, P], BF16)
-        nc.vector.memset(ones[:], 1.0)
-        bias_rows = keep.tile([P, (GATES - FIRST_BIAS_ROW_GATE) * H], BF16)
-        nc.vector.memset(bias_rows[:], 0.0)
-        nc.sync.dma_start(out=bias_rows[0:1, :], in_=bias[FIRST_BIAS_ROW_GATE * H :].unsqueeze(0))
+        first_row = const.tile([P, P], BF16)
+        nc.vector.memset(first_row[:], 0.0)
+        nc.vector.memset(first_row[0:1, :], 1.0)
+        bias_rows = keep.tile([P, GATES * H], BF16)
+
+        def load_bias(position):
+            units = slice(GATE_ORDER[position] * H, (GATE_ORDER[position] + 1) * H)
+            nc.sync.dma_start(out=bias_rows[:, units], in_=bias[units].partition_broadcast(P))
+
+        load_bias(0)
 
         waiting = []
         for i, name in enumerate(("x", "h")):
@@ -484,6 +497,8 @@ def tile_hyperlstmcell_pb_kernel(
                 if t == 4 * position - 6:
                     for name in ("x", "h", "b"):
                         load_small_weight(position, name)
+            if t in (2, 6, 10):
+                load_bias((t + 2) // 4)
             if t == 11:
                 shared = big_rows.tile([P, 4, K], BF16, name="big")
                 for i, name in enumerate(("x", "h", "b")):
@@ -510,7 +525,11 @@ def tile_hyperlstmcell_pb_kernel(
             if is_tile:
                 multiply(t, "x")
                 multiply(t, "h")
-            for q in quantised:
+            for q in quantised[:1]:
+                quantise_step(q)
+            if 0 <= t < VECTOR_BIAS_TILES:
+                add_bias_on_vector(t)
+            for q in quantised[1:]:
                 quantise_step(q)
             for name, g, grouped in act_waiting:
                 quantise_act(name, 2 * P, g, grouped)
@@ -519,12 +538,19 @@ def tile_hyperlstmcell_pb_kernel(
             for b in products:
                 gate_product(*b)
 
+            for m in range(BATCH_TILES):
+                if t == back_slot(m):
+                    cell_back(m)
+
             matmuls = []
             if z_tile:
                 matmuls += [(start_z, (t + 2, "x")), (start_z, (t + 2, "h"))]
             if is_tile:
-                matmuls += [(start_offset, (t,)), (add_bias, (t,))]
+                matmuls += [(start_offset, (t,))] + ([(add_bias, (t,))] if t >= VECTOR_BIAS_TILES else [])
+            if 0 <= t + 1 < N_TILES:
+                matmuls += [(start_product, (t + 1, name)) for name in ("x", "h")]
             copies = [(copy_z, (t + 2, name)) for name in ("x", "h")] if z_tile else []
+            copies.append((start_stats, (done_rows,)))
             transposes = [(turn_step, (q, pair, False)) for q in turned for pair in range(2)]
             transposes += [(gate_bank, b) for b in gate_banks if bank_slot(*b) == t]
             for position in range(1, GATES):
@@ -540,20 +566,15 @@ def tile_hyperlstmcell_pb_kernel(
             if t in (13, 14):
                 name = ("x", "h")[t - 13]
                 act_waiting = [(name, g, turn_act(name, g, False)) for g in range(PASSES)]
-            for m in range(BATCH_TILES):
-                if t == back_slot(m):
-                    cell_back(m)
-            if 0 <= t + 1 < N_TILES:
-                start_products(t + 1)
 
-            for m in range(BATCH_TILES):
-                if t == back_slot(m) + 3:
-                    nc.scalar.activation(out=cells[m]["values"][:], in_=cells[m]["new_c"][:], func=ACT.Tanh)
-                if t == norm_slot(GATES - 1, m) + 1:
-                    values = rows[GATES - 1, m]["values"]
-                    nc.scalar.activation(out=values[:], in_=values[:], func=ACT.Sigmoid)
-            for row in done_rows:
-                start_stats(row)
+            for half in range(HALVES):
+                units = slice(half * ROWS, (half + 1) * ROWS)
+                for m in range(BATCH_TILES):
+                    if t == back_slot(m) + 3:
+                        nc.scalar.activation(out=cells[m]["values"][:, units], in_=cells[m]["new_c"][:, units], func=ACT.Tanh)
+                    if t == norm_slot(GATES - 1, m) + 1:
+                        values = rows[GATES - 1, m]["values"][:, units]
+                        nc.scalar.activation(out=values, in_=values, func=ACT.Sigmoid)
 
             if is_tile:
                 add_products(t)
@@ -562,7 +583,7 @@ def tile_hyperlstmcell_pb_kernel(
                 if t == norm_slot(*row):
                     if GATE_ORDER[row[0]] == GATE_O:
                         centre(rows[row], "gain_o")
-                        normed.append((shift, (rows[row]["values"][:], rows[row], "shift_o")))
+                        normed += [(shift, (rows[row]["values"], rows[row], "shift_o", half)) for half in range(HALVES)]
                     else:
                         normalise(rows[row])
             for m in range(BATCH_TILES):

@@ -89,6 +89,15 @@ def new_h_slot(m):
     return max(back_slot(m) + 3, norm_slot(GATES - 1, m) + 1) + 1
 
 
+def sums_on_tensor(t):
+    return t in [norm_slot(GATES - 1, m) for m in range(BATCH_TILES)] + [back_slot(m) + 2 for m in range(BATCH_TILES)]
+
+
+def parts(m):
+    count = HALVES if m == BATCH_TILES - 1 else 1
+    return [slice(i * (H // count), (i + 1) * (H // count)) for i in range(count)]
+
+
 LAST_SLOT = new_h_slot(BATCH_TILES - 1)
 
 
@@ -233,6 +242,14 @@ def tile_hyperlstmcell_pb_kernel(
         def start_z(t, name):
             position, half, m = TILES[t]
             z = tiles.setdefault(t, {})["z_" + name] = psum_out.tile([P, ROWS], F32, name="z_" + name)
+            if sums_on_tensor(t):
+                for i in range(ROWS // P):
+                    first_unit = half * ROWS + i * P
+                    nc.tensor.matmul(
+                        out=z[:, i * P : (i + 1) * P], lhsT=small_t[position, name][:, first_unit : first_unit + P],
+                        rhs=emb_t[name][:, GATE_ORDER[position], m * P : (m + 1) * P], start=True, stop=True,
+                    )
+                return
             nc.tensor.matmul(
                 out=z[:], lhsT=emb_t[name][:, GATE_ORDER[position], m * P : (m + 1) * P],
                 rhs=small_t[position, name][:, half * ROWS : (half + 1) * ROWS], start=True, stop=True,
@@ -248,6 +265,20 @@ def tile_hyperlstmcell_pb_kernel(
             samples = slice(m * P, (m + 1) * P)
             half_gate = HALVES * position + half
             product = tiles[t]["product_" + name] = psum_out.tile([P, ROWS], F32, name="product_" + name)
+            if sums_on_tensor(t):
+                for i in range(ROWS // P):
+                    block = slice(i * P, (i + 1) * P)
+                    for g in range(PASSES):
+                        nc.tensor.matmul_mx(
+                            out=product[:, block],
+                            lhsT=codes[half_gate, name][:, g, block].bitcast(FP8X4),
+                            lhsT_scale=scales[half_gate][scale_row(name, g) : P, block],
+                            rhs=codes["act", name][:, g, samples].bitcast(FP8X4),
+                            rhs_scale=scales["act"][scale_row(name, g) : P, samples],
+                            start=(g == 0),
+                            stop=(g == PASSES - 1),
+                        )
+                return
             for g in range(PASSES):
                 nc.tensor.matmul_mx(
                     out=product[:],
@@ -273,8 +304,17 @@ def tile_hyperlstmcell_pb_kernel(
             first_unit = GATE_ORDER[position] * H + half * ROWS
             nc.tensor.matmul(
                 out=tiles[t]["z_b"][:], lhsT=first_row[:], rhs=bias_rows[:, first_unit : first_unit + ROWS],
-                start=False, stop=True,
+                start=False, stop=not sums_on_tensor(t),
             )
+
+        def add_transposed(t):
+            for name in ("x", "h"):
+                for i in range(ROWS // P):
+                    block = slice(i * P, (i + 1) * P)
+                    nc.tensor.matmul(
+                        out=tiles[t]["z_b"][:, block], lhsT=tiles[t]["term_" + name][:, block], rhs=ident_f32[:],
+                        is_transpose=True, start=False, stop=(name == "h" and i == ROWS // P - 1),
+                    )
 
         def add_bias_on_vector(t):
             position, half, m = TILES[t]
@@ -301,6 +341,12 @@ def tile_hyperlstmcell_pb_kernel(
                     "values": pre_pool.tile([P, H], F32, name="pre"), "sums": sums_pool.tile([P, HALVES], F32, name="sums"),
                 }
             row = rows[position, m]
+            if sums_on_tensor(t):
+                nc.scalar.activation(
+                    out=row["values"][:, half * ROWS : (half + 1) * ROWS], in_=tiles[t]["z_b"][:], func=ACT.Identity,
+                    accum_out=row["sums"][:, half : half + 1],
+                )
+                return
             nc.vector.scalar_tensor_tensor(
                 out=row["values"][:, half * ROWS : (half + 1) * ROWS], in0=tiles[t]["z_b"][:], scalar=1.0,
                 in1=tiles[t]["term_x"][:], op0=ALU.mult, op1=ALU.add, accum_out=row["sums"][:, half : half + 1],
@@ -394,31 +440,29 @@ def tile_hyperlstmcell_pb_kernel(
                     accum_out=row["sums"][:, half : half + 1],
                 )
 
-        def centre(row, gain):
+        def centre(out, row, gain):
             nc.vector.scalar_tensor_tensor(
-                out=row["values"][:], in0=row["values"][:], scalar=row["neg_mean"], in1=unit_vectors[gain][:],
+                out=out[:], in0=row["values"][:], scalar=row["neg_mean"], in1=unit_vectors[gain][:],
                 op0=ALU.add, op1=ALU.mult,
             )
 
-        def shift(out, row, vector, half):
-            units = slice(half * ROWS, (half + 1) * ROWS)
+        def shift(out, row, vector, units):
             nc.vector.scalar_tensor_tensor(
-                out=out[:, units], in0=row["values"][:, units], scalar=row["inv_std"], in1=unit_vectors[vector][:, units],
+                out=out[:, units], in0=out[:, units], scalar=row["inv_std"], in1=unit_vectors[vector][:, units],
                 op0=ALU.mult, op1=ALU.add,
             )
 
         def shift_cell(m):
-            new_c = cells[m]["new_c"] = big_rows.tile([P, H], F32, name="new_c", tag="big")
-            for half in range(HALVES):
-                shift(new_c, cells[m], "shift_c", half)
-            nc.sync.dma_start(out=out_1[m * P : (m + 1) * P, :], in_=new_c[:])
+            new_c = cells[m]["new_c"]
+            for units in parts(m):
+                shift(new_c, cells[m], "shift_c", units)
+                nc.sync.dma_start(out=out_1[m * P : (m + 1) * P, units], in_=new_c[:, units])
 
         def finish_h(m):
             values = cells[m]["values"]
-            for half in range(HALVES):
-                units = slice(half * ROWS, (half + 1) * ROWS)
+            for units in parts(m):
                 nc.vector.tensor_tensor(
-                    out=values[:, units], in0=rows[GATES - 1, m]["values"][:, units], in1=values[:, units], op=ALU.mult,
+                    out=values[:, units], in0=rows[GATES - 1, m]["normed"][:, units], in1=values[:, units], op=ALU.mult,
                 )
                 nc.sync.dma_start(out=out_0[m * P : (m + 1) * P, units], in_=values[:, units])
 
@@ -547,8 +591,9 @@ def tile_hyperlstmcell_pb_kernel(
                 matmuls += [(start_z, (t + 2, "x")), (start_z, (t + 2, "h"))]
             if is_tile:
                 matmuls += [(start_offset, (t,))] + ([(add_bias, (t,))] if t >= VECTOR_BIAS_TILES else [])
-            if 0 <= t + 1 < N_TILES:
-                matmuls += [(start_product, (t + 1, name)) for name in ("x", "h")]
+            if is_tile and sums_on_tensor(t):
+                matmuls.append((add_transposed, (t,)))
+            mx_passes = [(start_product, (t + 1, name)) for name in ("x", "h")] if 0 <= t + 1 < N_TILES else []
             copies = [(copy_z, (t + 2, name)) for name in ("x", "h")] if z_tile else []
             copies.append((start_stats, (done_rows,)))
             transposes = [(turn_step, (q, pair, False)) for q in turned for pair in range(2)]
@@ -558,37 +603,39 @@ def tile_hyperlstmcell_pb_kernel(
                     transposes.append((turn_small_weight, (position, ("x", "h", "b")[t - (4 * position - 5)])))
             if t in (12, 13):
                 transposes += [(turn_embedding, (name, 2 * P)) for name in (("x", "h") if t == 12 else ("b",))]
-            while matmuls or transposes or copies:
-                for work_list in (matmuls, transposes, copies):
-                    for function, arguments in work_list[:1]:
-                        function(*arguments)
+            while matmuls or copies:
+                for function, arguments in matmuls[:1] + transposes[:1] + copies[:1]:
+                    function(*arguments)
                 matmuls, transposes, copies = matmuls[1:], transposes[1:], copies[1:]
+            for function, arguments in mx_passes[:1] + transposes + mx_passes[1:]:
+                function(*arguments)
             if t in (13, 14):
                 name = ("x", "h")[t - 13]
                 act_waiting = [(name, g, turn_act(name, g, False)) for g in range(PASSES)]
 
-            for half in range(HALVES):
-                units = slice(half * ROWS, (half + 1) * ROWS)
-                for m in range(BATCH_TILES):
+            for m in range(BATCH_TILES):
+                for units in parts(m):
                     if t == back_slot(m) + 3:
                         nc.scalar.activation(out=cells[m]["values"][:, units], in_=cells[m]["new_c"][:, units], func=ACT.Tanh)
                     if t == norm_slot(GATES - 1, m) + 1:
-                        values = rows[GATES - 1, m]["values"][:, units]
+                        values = rows[GATES - 1, m]["normed"][:, units]
                         nc.scalar.activation(out=values, in_=values, func=ACT.Sigmoid)
 
-            if is_tile:
+            if is_tile and not sums_on_tensor(t):
                 add_products(t)
             normed = []
             for row in all_rows:
                 if t == norm_slot(*row):
                     if GATE_ORDER[row[0]] == GATE_O:
-                        centre(rows[row], "gain_o")
-                        normed += [(shift, (rows[row]["values"], rows[row], "shift_o", half)) for half in range(HALVES)]
+                        rows[row]["normed"] = pre_pool.tile([P, H], F32, name="normed_o", tag="pre")
+                        centre(rows[row]["normed"], rows[row], "gain_o")
+                        normed += [(shift, (rows[row]["normed"], rows[row], "shift_o", units)) for units in parts(row[1])]
                     else:
                         normalise(rows[row])
             for m in range(BATCH_TILES):
                 if t == back_slot(m) + 2:
-                    centre(cells[m], "gain_c")
+                    cells[m]["new_c"] = big_rows.tile([P, H], F32, name="new_c", tag="big")
+                    centre(cells[m]["new_c"], cells[m], "gain_c")
                     normed.append((shift_cell, (m,)))
             if is_tile:
                 finish_tile(t)

@@ -72,7 +72,7 @@ def blocks_per_bank(group):
 
 
 def norm_slot(position, m):
-    return row_slot(position, m) + 2
+    return row_slot(position, m) + (2 if m in GROUPS[0] else 3)
 
 
 def bank_slot(group, position, k):
@@ -86,11 +86,11 @@ def back_slot(m):
 
 
 def new_h_slot(m):
-    return max(back_slot(m) + 3, norm_slot(GATES - 1, m) + 1) + 1
+    return max(back_slot(m) + 4, norm_slot(GATES - 1, m) + 1) + 1
 
 
 def sums_on_tensor(t):
-    return t in [norm_slot(GATES - 1, m) for m in range(BATCH_TILES)] + [back_slot(m) + 2 for m in range(BATCH_TILES)]
+    return t in [norm_slot(GATES - 1, m) for m in range(BATCH_TILES)] + [back_slot(m) + 3 for m in range(BATCH_TILES)]
 
 
 def parts(m):
@@ -554,7 +554,7 @@ def tile_hyperlstmcell_pb_kernel(
                     act_rows[name] = shared[:, 2 * i : 2 * i + 2, :]
                     load_act(name, 2 * P)
             for m in range(BATCH_TILES):
-                if t == row_slot(GATE_ORDER.index(GATE_F), m) - 2:
+                if t == norm_slot(GATE_ORDER.index(GATE_F), m):
                     c_rows[m] = c_pool.tile([P, H], BF16, name="c_rows")
                     nc.sync.dma_start(out=c_rows[m][:], in_=c[m * P : (m + 1) * P, :])
             if t == 10:
@@ -615,7 +615,7 @@ def tile_hyperlstmcell_pb_kernel(
 
             for m in range(BATCH_TILES):
                 for units in parts(m):
-                    if t == back_slot(m) + 3:
+                    if t == back_slot(m) + 4:
                         nc.scalar.activation(out=cells[m]["values"][:, units], in_=cells[m]["new_c"][:, units], func=ACT.Tanh)
                     if t == norm_slot(GATES - 1, m) + 1:
                         values = rows[GATES - 1, m]["normed"][:, units]
@@ -633,7 +633,7 @@ def tile_hyperlstmcell_pb_kernel(
                     else:
                         normalise(rows[row])
             for m in range(BATCH_TILES):
-                if t == back_slot(m) + 2:
+                if t == back_slot(m) + 3:
                     cells[m]["new_c"] = big_rows.tile([P, H], F32, name="new_c", tag="big")
                     centre(cells[m]["new_c"], cells[m], "gain_c")
                     normed.append((shift_cell, (m,)))

@@ -50,6 +50,7 @@ LOAD_LEAD = 1
 VECTOR_BIAS_TILES = N_STEPS // STEPS_PER_SLOT - 4
 BANK_COLUMNS = 512
 BANKS_PER_SLOT = 1
+CELL_LAG = 3
 BACK_SPACING = 3
 
 FLOPS = 2 * (2 * B * K * GATES * H) + 3 * (2 * B * E * GATES * H)
@@ -86,11 +87,11 @@ def back_slot(m):
 
 
 def new_h_slot(m):
-    return max(back_slot(m) + 4, norm_slot(GATES - 1, m) + 1) + 1
+    return max(back_slot(m) + CELL_LAG + 1, norm_slot(GATES - 1, m) + 1) + 1
 
 
 def sums_on_tensor(t):
-    return t in [norm_slot(GATES - 1, m) for m in range(BATCH_TILES)] + [back_slot(m) + 3 for m in range(BATCH_TILES)]
+    return t in [norm_slot(GATES - 1, m) for m in range(BATCH_TILES)] + [back_slot(m) + CELL_LAG for m in range(BATCH_TILES)]
 
 
 def parts(m):
@@ -120,12 +121,11 @@ def tile_hyperlstmcell_pb_kernel(
         work = ctx.enter_context(tc.tile_pool(name="work", bufs=2))
         z_pool = ctx.enter_context(tc.tile_pool(name="z_sb", bufs=2))
         pre_pool = ctx.enter_context(tc.tile_pool(name="pre", bufs=6))
-        sums_pool = ctx.enter_context(tc.tile_pool(name="sums", bufs=6))
         block_pool = ctx.enter_context(tc.tile_pool(name="block", bufs=2))
         cell_rows = ctx.enter_context(tc.tile_pool(name="cell_rows", bufs=2))
         scratch = ctx.enter_context(tc.tile_pool(name="scratch", bufs=1))
         c_pool = ctx.enter_context(tc.tile_pool(name="c_rows", bufs=2))
-        stats = ctx.enter_context(tc.tile_pool(name="stats", bufs=8))
+        stats = ctx.enter_context(tc.tile_pool(name="stats", bufs=10))
         psum_out = ctx.enter_context(tc.psum_pool(name="psum_out", bufs=1))
         psum_turn = ctx.enter_context(tc.psum_pool(name="psum_turn", bufs=3))
 
@@ -135,8 +135,6 @@ def tile_hyperlstmcell_pb_kernel(
         make_identity(nc, ident_bf16[:])
         exp_half = const.tile([P, 1], F32)
         nc.vector.memset(exp_half[:], 0.5)
-        exp_minus_one = const.tile([P, 1], F32)
-        nc.vector.memset(exp_minus_one[:], -1.0)
 
         tiles, rows, cells, step_rows, step_grouped = {}, {}, {}, {}, {}
         act_rows, emb_rows, c_rows, emb_t, small_t, unit_vectors = {}, {}, {}, {}, {}, {}
@@ -337,9 +335,7 @@ def tile_hyperlstmcell_pb_kernel(
         def finish_tile(t):
             position, half, m = TILES[t]
             if half == 0:
-                rows[position, m] = {
-                    "values": pre_pool.tile([P, H], F32, name="pre"), "sums": sums_pool.tile([P, HALVES], F32, name="sums"),
-                }
+                rows[position, m] = new_row(pre_pool.tile([P, H], F32, name="pre"))
             row = rows[position, m]
             if sums_on_tensor(t):
                 nc.scalar.activation(
@@ -352,28 +348,36 @@ def tile_hyperlstmcell_pb_kernel(
                 in1=tiles[t]["term_x"][:], op0=ALU.mult, op1=ALU.add, accum_out=row["sums"][:, half : half + 1],
             )
 
+        def new_row(values):
+            numbers = stats.tile([P, 5], F32, name="numbers")
+            by_gpsimd = stats.tile([P, 2], F32, name="by_gpsimd")
+            return {
+                "values": values, "sums": numbers[:, 0:HALVES], "sum_sq": numbers[:, 2:3], "std_eps": numbers[:, 3:4],
+                "inv_std": numbers[:, 4:5], "neg_mean": by_gpsimd[:, 0:1], "root": by_gpsimd[:, 1:2],
+            }
+
+        def negate_mean(row):
+            nc.gpsimd.tensor_scalar(
+                out=row["neg_mean"], in0=row["sums"][:, 0:1], scalar1=row["sums"][:, 1:2], scalar2=-1.0 / H,
+                op0=ALU.add, op1=ALU.mult,
+            )
+
         def start_stats(some_rows):
-            for row in some_rows:
-                numbers = stats.tile([P, 5], F32, name="numbers")
-                row["neg_mean"], row["sum_sq"], row["root"], row["std_eps"], row["inv_std"] = [
-                    numbers[:, i : i + 1] for i in range(5)
-                ]
-                nc.gpsimd.tensor_scalar(
-                    out=row["neg_mean"], in0=row["sums"][:, 0:1], scalar1=row["sums"][:, 1:2], scalar2=-1.0 / H,
-                    op0=ALU.add, op1=ALU.mult,
-                )
             for row in some_rows:
                 squares = scratch.tile([P, H], BF16, name="squares")
                 nc.scalar.activation(
                     out=squares[:], in_=row["values"][:], func=ACT.Square, bias=row["neg_mean"], scale=1.0,
                     accum_out=row["sum_sq"],
                 )
-            for row in some_rows:
                 nc.gpsimd.tensor_tensor(out=row["root"], in0=row["sum_sq"], in1=exp_half[:], op=ALU.pow)
-                nc.gpsimd.tensor_scalar(
-                    out=row["std_eps"], in0=row["root"], scalar1=1.0 / math.sqrt(H - 1), scalar2=EPS, op0=ALU.mult, op1=ALU.add,
-                )
-                nc.gpsimd.tensor_tensor(out=row["inv_std"], in0=row["std_eps"], in1=exp_minus_one[:], op=ALU.pow)
+
+        def deviation(row):
+            nc.vector.tensor_scalar(
+                out=row["std_eps"], in0=row["root"], scalar1=1.0 / math.sqrt(H - 1), scalar2=EPS, op0=ALU.mult, op1=ALU.add,
+            )
+
+        def invert(row):
+            nc.vector.reciprocal(out=row["inv_std"], in_=row["std_eps"])
 
         def normalise(row):
             nc.vector.tensor_scalar(
@@ -423,9 +427,7 @@ def tile_hyperlstmcell_pb_kernel(
                 nc.vector.tensor_tensor(out=term, in0=c_bank[:], in1=activated[position, k][:], op=ALU.mult)
 
         def cell_back(m):
-            row = cells[m] = {
-                "values": cell_rows.tile([P, H], F32, name="cell_row"), "sums": sums_pool.tile([P, HALVES], F32, name="cell_sums"),
-            }
+            row = cells[m] = new_row(cell_rows.tile([P, H], F32, name="cell_row"))
             for half in range(HALVES):
                 bank = psum_turn.tile([P, ROWS], F32, tag="turned", name="turned_cell")
                 for i in range(ROWS // P):
@@ -475,10 +477,11 @@ def tile_hyperlstmcell_pb_kernel(
         for i, name in enumerate(("x", "h")):
             load_act(name, 0)
             load_step(PASSES * i)
-        for name in ("x", "h", "b"):
             load_embedding(name, 0)
             load_small_weight(0, name)
-        vector_rows = const.tile([P, P], BF16)
+        load_embedding("b", 0)
+        load_small_weight(0, "b")
+        vector_rows = scratch.tile([P, P], BF16, name="vector_rows", tag="squares")
         nc.vector.memset(vector_rows[:], 0.0)
         for i, vector in enumerate((ln_gamma, ln_beta)):
             nc.sync.dma_start(
@@ -511,11 +514,12 @@ def tile_hyperlstmcell_pb_kernel(
                 if len(waiting) > 1:
                     function, arguments = waiting.pop(0)
                     function(*arguments)
-        for function, arguments in waiting:
-            function(*arguments)
-        for name in ("x", "h", "b"):
             turn_embedding(name, 0)
             turn_small_weight(0, name)
+        for function, arguments in waiting:
+            function(*arguments)
+        turn_embedding("b", 0)
+        turn_small_weight(0, "b")
 
         unit_columns = const.tile([P, P], F32)
         vector_bank = psum_turn.tile([P, P], BF16, tag="turned", name="turned_vectors")
@@ -566,9 +570,19 @@ def tile_hyperlstmcell_pb_kernel(
 
             done_rows = [rows[row] for row in all_rows if row_slot(*row) == t - 1]
             done_rows += [cells[m] for m in range(BATCH_TILES) if t == back_slot(m) + 1]
+            due_rows = [rows[row] for row in all_rows if norm_slot(*row) == t]
+            due_rows += [cells[m] for m in range(BATCH_TILES) if t == back_slot(m) + CELL_LAG]
+            for row in done_rows:
+                negate_mean(row)
+
             if is_tile:
                 multiply(t, "x")
+            for row in due_rows:
+                deviation(row)
+            if is_tile:
                 multiply(t, "h")
+            for row in due_rows:
+                invert(row)
             for q in quantised[:1]:
                 quantise_step(q)
             if 0 <= t < VECTOR_BIAS_TILES:
@@ -615,7 +629,7 @@ def tile_hyperlstmcell_pb_kernel(
 
             for m in range(BATCH_TILES):
                 for units in parts(m):
-                    if t == back_slot(m) + 4:
+                    if t == back_slot(m) + CELL_LAG + 1:
                         nc.scalar.activation(out=cells[m]["values"][:, units], in_=cells[m]["new_c"][:, units], func=ACT.Tanh)
                     if t == norm_slot(GATES - 1, m) + 1:
                         values = rows[GATES - 1, m]["normed"][:, units]
@@ -633,7 +647,7 @@ def tile_hyperlstmcell_pb_kernel(
                     else:
                         normalise(rows[row])
             for m in range(BATCH_TILES):
-                if t == back_slot(m) + 3:
+                if t == back_slot(m) + CELL_LAG:
                     cells[m]["new_c"] = big_rows.tile([P, H], F32, name="new_c", tag="big")
                     centre(cells[m]["new_c"], cells[m], "gain_c")
                     normed.append((shift_cell, (m,)))

import math
from contextlib import ExitStack

import concourse.mybir as mybir
from concourse.masks import make_identity

F32 = mybir.dt.float32
BF16 = mybir.dt.bfloat16
U32 = mybir.dt.uint32
U8 = mybir.dt.uint8
FP8X4 = mybir.dt.float8_e4m3fn_x4
ACT = mybir.ActivationFunctionType
ALU = mybir.AluOpType

P = 128
B = 512
K = 1024
H = 1024
E = 128
GATES = 4
BATCH_TILES = B // P
GROUPS = ((0, 1), (2,), (3,))
K_PASS = 4 * P
PASSES = K // K_PASS
ROWS = 512
HALVES = H // ROWS
UNIT_BLOCKS = H // P
EPS = 1e-6

GATE_I, GATE_F, GATE_G, GATE_O = 0, 1, 2, 3
GATE_ORDER = (GATE_I, GATE_G, GATE_F, GATE_O)
TILES = [
    (position, half, m)
    for group, positions in (
        (GROUPS[0], range(GATES)), (GROUPS[1], range(GATES - 1)), (GROUPS[2], range(GATES - 1)),
        (GROUPS[1], (GATES - 1,)), (GROUPS[2], (GATES - 1,)),
    )
    for position in positions for half in range(HALVES) for m in group
]
N_TILES = len(TILES)

STEPS_PER_HALF_GATE = 2 * PASSES
HALF_GATES = GATES * HALVES
N_STEPS = HALF_GATES * STEPS_PER_HALF_GATE
SCALE_ROWS = 4
STEPS_PER_SLOT = STEPS_PER_HALF_GATE // len(GROUPS[0])
TURN_LEAD = 1
LOAD_LEAD = 1

VECTOR_BIAS_TILES = N_STEPS // STEPS_PER_SLOT - 4
BANK_COLUMNS = 512
BANKS_PER_SLOT = 1
CELL_LAG = 3
BACK_SPACING = 3

FLOPS = 2 * (2 * B * K * GATES * H) + 3 * (2 * B * E * GATES * H)


def row_slot(position, m):
    return TILES.index((position, HALVES - 1, m))


def scale_row(name, g):
    return SCALE_ROWS * (PASSES * ("x", "h").index(name) + g)


def quantise_slot(q):
    return q // STEPS_PER_SLOT - 3


def blocks_per_bank(group):
    return BANK_COLUMNS // (P * len(group))


def norm_slot(position, m):
    return row_slot(position, m) + (2 if m in GROUPS[0] else 3)


def bank_slot(group, position, k):
    return norm_slot(position, group[-1]) + 1 + k // BANKS_PER_SLOT


def back_slot(m):
    group = [group for group in GROUPS if m in group][0]
    last_bank = UNIT_BLOCKS // blocks_per_bank(group) - 1
    return bank_slot(group, GATE_ORDER.index(GATE_F), last_bank) + 2 + BACK_SPACING * group.index(m)


def new_h_slot(m):
    return max(back_slot(m) + CELL_LAG + 1, norm_slot(GATES - 1, m) + 1) + 1


def sums_on_tensor(t):
    return t in [norm_slot(GATES - 1, m) for m in range(BATCH_TILES)] + [back_slot(m) + CELL_LAG for m in range(BATCH_TILES)]


def parts(m):
    count = HALVES if m == BATCH_TILES - 1 else 1
    return [slice(i * (H // count), (i + 1) * (H // count)) for i in range(count)]


LAST_SLOT = new_h_slot(BATCH_TILES - 1)


def tile_hyperlstmcell_pb_kernel(
    tc, x, h, c, emb_h, emb_x, emb_b, Wsh, Wsx, Wsb, Wih, Whh, bias,
    ln_gamma, ln_beta, lnc_gamma, lnc_beta, out_0, out_1,
):
    nc = tc.nc
    activation = {"x": x, "h": h}
    big_weight = {"x": Wih, "h": Whh}
    small_weight = {"x": Wsx, "h": Wsh, "b": Wsb}
    embedding = {"x": emb_x, "h": emb_h, "b": emb_b}

    with ExitStack() as ctx:
        const = ctx.enter_context(tc.tile_pool(name="const", bufs=1))
        keep = ctx.enter_context(tc.tile_pool(name="keep", bufs=1))
        big_rows = ctx.enter_context(tc.tile_pool(name="big_rows", bufs=2))
        small_rows = ctx.enter_context(tc.tile_pool(name="small_rows", bufs=3))
        grouped_pool = ctx.enter_context(tc.tile_pool(name="grouped", bufs=3))
        work = ctx.enter_context(tc.tile_pool(name="work", bufs=2))
        z_pool = ctx.enter_context(tc.tile_pool(name="z_sb", bufs=2))
        pre_pool = ctx.enter_context(tc.tile_pool(name="pre", bufs=6))
        block_pool = ctx.enter_context(tc.tile_pool(name="block", bufs=2))
        cell_rows = ctx.enter_context(tc.tile_pool(name="cell_rows", bufs=2))
        scratch = ctx.enter_context(tc.tile_pool(name="scratch", bufs=1))
        c_pool = ctx.enter_context(tc.tile_pool(name="c_rows", bufs=2))
        stats = ctx.enter_context(tc.tile_pool(name="stats", bufs=10))
        psum_out = ctx.enter_context(tc.psum_pool(name="psum_out", bufs=1))
        psum_turn = ctx.enter_context(tc.psum_pool(name="psum_turn", bufs=3))

        ident_f32 = const.tile([P, P], F32)
        make_identity(nc, ident_f32[:])
        ident_bf16 = const.tile([P, P], BF16)
        make_identity(nc, ident_bf16[:])
        exp_half = const.tile([P, 1], F32)
        nc.vector.memset(exp_half[:], 0.5)

        tiles, rows, cells, step_rows, step_grouped = {}, {}, {}, {}, {}
        act_rows, emb_rows, c_rows, emb_t, small_t, unit_vectors = {}, {}, {}, {}, {}, {}
        codes, scales = {}, {}

        def load_act(name, first):
            if first == 0:
                act_rows[name] = pre_pool.tile([P, 2, K], BF16, name="act_rows_" + name, tag="pre")[:]
            nc.sync.dma_start(
                out=act_rows[name], in_=activation[name][first : first + 2 * P, :].rearrange("(r p) k -> p r k", p=P),
            )

        def load_embedding(name, first):
            if first == 0:
                emb_rows[name] = pre_pool.tile([P, 2, GATES * E], BF16, name="emb_rows_" + name, tag="pre")[:]
            nc.sync.dma_start(
                out=emb_rows[name], in_=embedding[name][first : first + 2 * P].rearrange("(m p) g e -> p m (g e)", p=P),
            )

        def load_step(q):
            half_gate, name = q // STEPS_PER_HALF_GATE, ("x", "h")[(q % STEPS_PER_HALF_GATE) // PASSES]
            first_row = GATE_ORDER[half_gate // HALVES] * H + half_gate % HALVES * ROWS
            step_rows[q // PASSES] = big_rows.tile([P, ROWS // P, K], BF16, name="big")
            nc.sync.dma_start(
                out=step_rows[q // PASSES][:],
                in_=big_weight[name][first_row : first_row + ROWS, :].rearrange("(r p) k -> p r k", p=P),
            )

        def load_small_weight(position, name):
            small_t[position, name] = small_rows.tile([P, UNIT_BLOCKS, E], BF16, name="small_rows")
            nc.sync.dma_start(
                out=small_t[position, name][:],
                in_=small_weight[name][GATE_ORDER[position]].rearrange("(j p) e -> p j e", p=P),
            )

        def turn_rows(rows_sb, first, g, grouped, pair, on_vector):
            bank = psum_turn.tile([P, 2, 2 * P], F32, tag="turned", name="turned_rows")
            for u in range(2):
                for r in range(2):
                    words = slice(2 * P * g + u, 2 * P * (g + 1), 2)
                    nc.tensor.transpose(
                        bank[:, u, r * P : (r + 1) * P], rows_sb[:, first + r, :].bitcast(F32)[:, words], ident_f32[:],
                    )
            target = grouped[:].bitcast(F32).rearrange("p (r u) -> p r u", u=2)[:, 2 * P * pair : 2 * P * (pair + 1), :]
            if on_vector:
                nc.vector.tensor_copy(out=target, in_=bank[:].rearrange("p u r -> p r u"))
            else:
                nc.scalar.copy(out=target, in_=bank[:].rearrange("p u r -> p r u"))

        for name in ("x", "h"):
            codes["act", name] = keep.tile([P, PASSES, B], U32, align_bytes=64, name="act_codes_" + name)
        scales["act"] = keep.tile([P, B], U8, align_bytes=64, name="act_scales")

        def turn_act(name, g, on_vector):
            grouped = grouped_pool.tile([P, 8 * P], BF16, align_bytes=64, name="act_grouped", tag="grouped")
            turn_rows(act_rows[name], 0, g, grouped, 0, on_vector)
            return grouped

        def quantise_act(name, first, g, grouped):
            samples = slice(first, first + 2 * P)
            nc.vector.quantize_mx(
                out=codes["act", name][:, g, samples].bitcast(FP8X4), scales=scales["act"][scale_row(name, g) : P, samples],
                in_=grouped[:],
            )

        def turn_step(q, pair, on_vector):
            if pair == 0:
                step_grouped[q] = grouped_pool.tile([P, 4 * ROWS], BF16, align_bytes=64, name="grouped")
            turn_rows(step_rows[q // PASSES], 2 * pair, q % PASSES, step_grouped[q], pair, on_vector)

        def quantise_step(q):
            half_gate, name, g = q // STEPS_PER_HALF_GATE, ("x", "h")[(q % STEPS_PER_HALF_GATE) // PASSES], q % PASSES
            if g == 0:
                codes[half_gate, name] = keep.tile([P, PASSES, ROWS], U32, align_bytes=64, name="codes_%s_%d" % (name, half_gate))
            if q % STEPS_PER_HALF_GATE == 0:
                scales[half_gate] = keep.tile([P, ROWS], U8, align_bytes=64, name="scales_%d" % half_gate)
            nc.vector.quantize_mx(
                out=codes[half_gate, name][:, g, :].bitcast(FP8X4),
                scales=scales[half_gate][scale_row(name, g) : P, :],
                in_=step_grouped[q][:],
            )

        def transpose_eight(blocks, dst, **shape):
            bank = psum_turn.tile([P, 8 * P], BF16, tag="turned", name="turned_eight")
            for i, block in enumerate(blocks):
                nc.tensor.transpose(bank[:, i * P : (i + 1) * P], block, ident_bf16[:])
            nc.scalar.copy(out=dst, in_=bank[:].rearrange("p (g b) -> p g b", **shape) if shape else bank[:])

        for name in ("x", "h", "b"):
            emb_t[name] = keep.tile([P, GATES, B], BF16, name="emb_t_" + name)

        def turn_embedding(name, first):
            transpose_eight(
                [emb_rows[name][:, i, gate * E : (gate + 1) * E] for gate in range(GATES) for i in range(2)],
                emb_t[name][:, :, first : first + 2 * P], g=GATES,
            )

        def turn_small_weight(position, name):
            rows_sb = small_t[position, name]
            small_t[position, name] = keep.tile([P, H], BF16, name="small_%s_%d" % (name, position))
            transpose_eight([rows_sb[:, j, :] for j in range(UNIT_BLOCKS)], small_t[position, name][:])

        def start_z(t, name):
            position, half, m = TILES[t]
            z = tiles.setdefault(t, {})["z_" + name] = psum_out.tile([P, ROWS], F32, name="z_" + name)
            if sums_on_tensor(t):
                for i in range(ROWS // P):
                    first_unit = half * ROWS + i * P
                    nc.tensor.matmul(
                        out=z[:, i * P : (i + 1) * P], lhsT=small_t[position, name][:, first_unit : first_unit + P],
                        rhs=emb_t[name][:, GATE_ORDER[position], m * P : (m + 1) * P], start=True, stop=True,
                    )
                return
            nc.tensor.matmul(
                out=z[:], lhsT=emb_t[name][:, GATE_ORDER[position], m * P : (m + 1) * P],
                rhs=small_t[position, name][:, half * ROWS : (half + 1) * ROWS], start=True, stop=True,
            )

        def copy_z(t, name):
            tile = tiles[t]
            tile["z_sb_" + name] = z_pool.tile([P, ROWS], F32, name="z_sb_" + name)
            nc.scalar.copy(out=tile["z_sb_" + name][:], in_=tile["z_" + name][:])

        def start_product(t, name):
            position, half, m = TILES[t]
            samples = slice(m * P, (m + 1) * P)
            half_gate = HALVES * position + half
            product = tiles[t]["product_" + name] = psum_out.tile([P, ROWS], F32, name="product_" + name)
            if sums_on_tensor(t):
                for i in range(ROWS // P):
                    block = slice(i * P, (i + 1) * P)
                    for g in range(PASSES):
                        nc.tensor.matmul_mx(
                            out=product[:, block],
                            lhsT=codes[half_gate, name][:, g, block].bitcast(FP8X4),
                            lhsT_scale=scales[half_gate][scale_row(name, g) : P, block],
                            rhs=codes["act", name][:, g, samples].bitcast(FP8X4),
                            rhs_scale=scales["act"][scale_row(name, g) : P, samples],
                            start=(g == 0),
                            stop=(g == PASSES - 1),
                        )
                return
            for g in range(PASSES):
                nc.tensor.matmul_mx(
                    out=product[:],
                    lhsT=codes["act", name][:, g, samples].bitcast(FP8X4),
                    lhsT_scale=scales["act"][scale_row(name, g) : P, samples],
                    rhs=codes[half_gate, name][:, g, :].bitcast(FP8X4),
                    rhs_scale=scales[half_gate][scale_row(name, g) : P, :],
                    start=(g == 0),
                    stop=(g == PASSES - 1),
                )

        def start_offset(t):
            position, half, m = TILES[t]
            z_b = tiles[t]["z_b"] = psum_out.tile([P, ROWS], F32, name="z_b")
            nc.tensor.matmul(
                out=z_b[:], lhsT=emb_t["b"][:, GATE_ORDER[position], m * P : (m + 1) * P],
                rhs=small_t[position, "b"][:, half * ROWS : (half + 1) * ROWS],
                start=True, stop=(t < VECTOR_BIAS_TILES),
            )

        def add_bias(t):
            position, half, m = TILES[t]
            first_unit = GATE_ORDER[position] * H + half * ROWS
            nc.tensor.matmul(
                out=tiles[t]["z_b"][:], lhsT=first_row[:], rhs=bias_rows[:, first_unit : first_unit + ROWS],
                start=False, stop=not sums_on_tensor(t),
            )

        def add_transposed(t):
            for name in ("x", "h"):
                for i in range(ROWS // P):
                    block = slice(i * P, (i + 1) * P)
                    nc.tensor.matmul(
                        out=tiles[t]["z_b"][:, block], lhsT=tiles[t]["term_" + name][:, block], rhs=ident_f32[:],
                        is_transpose=True, start=False, stop=(name == "h" and i == ROWS // P - 1),
                    )

        def add_bias_on_vector(t):
            position, half, m = TILES[t]
            first_unit, term = GATE_ORDER[position] * H + half * ROWS, tiles[t]["term_x"]
            nc.vector.tensor_tensor(
                out=term[:], in0=term[:], in1=bias_rows[:, first_unit : first_unit + ROWS], op=ALU.add,
            )

        def multiply(t, name):
            tile = tiles[t]
            tile["term_" + name] = work.tile([P, ROWS], F32, name="term_" + name)
            nc.vector.tensor_tensor(
                out=tile["term_" + name][:], in0=tile["product_" + name][:], in1=tile["z_sb_" + name][:], op=ALU.mult,
            )

        def add_products(t):
            tile = tiles[t]
            nc.vector.tensor_tensor(out=tile["term_x"][:], in0=tile["term_x"][:], in1=tile["term_h"][:], op=ALU.add)

        def finish_tile(t):
            position, half, m = TILES[t]
            if half == 0:
                rows[position, m] = new_row(pre_pool.tile([P, H], F32, name="pre"))
            row = rows[position, m]
            if sums_on_tensor(t):
                nc.scalar.activation(
                    out=row["values"][:, half * ROWS : (half + 1) * ROWS], in_=tiles[t]["z_b"][:], func=ACT.Identity,
                    accum_out=row["sums"][:, half : half + 1],
                )
                return
            nc.vector.scalar_tensor_tensor(
                out=row["values"][:, half * ROWS : (half + 1) * ROWS], in0=tiles[t]["z_b"][:], scalar=1.0,
                in1=tiles[t]["term_x"][:], op0=ALU.mult, op1=ALU.add, accum_out=row["sums"][:, half : half + 1],
            )

        def new_row(values):
            numbers = stats.tile([P, 5], F32, name="numbers")
            by_gpsimd = stats.tile([P, 2], F32, name="by_gpsimd")
            return {
                "values": values, "sums": numbers[:, 0:HALVES], "sum_sq": numbers[:, 2:3], "std_eps": numbers[:, 3:4],
                "inv_std": numbers[:, 4:5], "neg_mean": by_gpsimd[:, 0:1], "root": by_gpsimd[:, 1:2],
            }

        def negate_mean(row):
            nc.gpsimd.tensor_scalar(
                out=row["neg_mean"], in0=row["sums"][:, 0:1], scalar1=row["sums"][:, 1:2], scalar2=-1.0 / H,
                op0=ALU.add, op1=ALU.mult,
            )

        def start_stats(some_rows):
            for row in some_rows:
                squares = scratch.tile([P, H], BF16, name="squares")
                nc.scalar.activation(
                    out=squares[:], in_=row["values"][:], func=ACT.Square, bias=row["neg_mean"], scale=1.0,
                    accum_out=row["sum_sq"],
                )
                nc.gpsimd.tensor_tensor(out=row["root"], in0=row["sum_sq"], in1=exp_half[:], op=ALU.pow)

        def deviation(row):
            nc.vector.tensor_scalar(
                out=row["std_eps"], in0=row["root"], scalar1=1.0 / math.sqrt(H - 1), scalar2=EPS, op0=ALU.mult, op1=ALU.add,
            )

        def invert(row):
            nc.vector.reciprocal(out=row["inv_std"], in_=row["std_eps"])

        def normalise(row):
            nc.vector.tensor_scalar(
                out=row["values"][:], in0=row["values"][:], scalar1=row["neg_mean"], scalar2=row["inv_std"],
                op0=ALU.add, op1=ALU.mult,
            )

        def cell_columns(group):
            return slice(group[0] % 2 * P, group[0] % 2 * P + P * len(group))

        def bank_blocks(group, k):
            return range(k * blocks_per_bank(group), (k + 1) * blocks_per_bank(group))

        def gate_bank(group, position, k):
            gate, blocks, samples = GATE_ORDER[position], bank_blocks(group, k), P * len(group)
            bank = psum_turn.tile([P, len(blocks), samples], F32, tag="turned", name="turned_gate")
            for i, j in enumerate(blocks):
                for s, m in enumerate(group):
                    nc.tensor.transpose(
                        bank[:, i, s * P : (s + 1) * P], rows[position, m]["values"][:, j * P : (j + 1) * P], ident_f32[:],
                    )
            if gate == GATE_I:
                target = cell_i[:, blocks[0] : blocks[-1] + 1, cell_columns(group)]
            else:
                activated[position, k] = block_pool.tile([P, len(blocks), samples], F32, name="activated")
                target = activated[position, k][:]
            for i, j in enumerate(blocks):
                column = gate * UNIT_BLOCKS + j
                nc.scalar.activation(
                    out=target[:, i, :], in_=bank[:, i, :], func=ACT.Tanh if gate == GATE_G else ACT.Sigmoid,
                    scale=unit_columns[:, column : column + 1],
                    bias=unit_columns[:, GATES * UNIT_BLOCKS + column : GATES * UNIT_BLOCKS + column + 1],
                )

        def gate_product(group, position, k):
            gate, blocks, samples = GATE_ORDER[position], bank_blocks(group, k), P * len(group)
            term = (cell_f if gate == GATE_F else cell_i)[:, blocks[0] : blocks[-1] + 1, cell_columns(group)]
            if gate == GATE_G:
                nc.vector.tensor_tensor(out=term, in0=term, in1=activated[position, k][:], op=ALU.mult)
            if gate == GATE_F:
                c_bank = psum_turn.tile([P, len(blocks), samples], BF16, tag="turned", name="turned_c")
                for i, j in enumerate(blocks):
                    for s, m in enumerate(group):
                        nc.tensor.transpose(
                            c_bank[:, i, s * P : (s + 1) * P], c_rows[m][:, j * P : (j + 1) * P], ident_bf16[:],
                        )
                nc.vector.tensor_tensor(out=term, in0=c_bank[:], in1=activated[position, k][:], op=ALU.mult)

        def cell_back(m):
            row = cells[m] = new_row(cell_rows.tile([P, H], F32, name="cell_row"))
            for half in range(HALVES):
                bank = psum_turn.tile([P, ROWS], F32, tag="turned", name="turned_cell")
                for i in range(ROWS // P):
                    for term in (cell_i, cell_f):
                        nc.tensor.matmul(
                            out=bank[:, i * P : (i + 1) * P],
                            lhsT=term[:, half * (ROWS // P) + i, m % 2 * P : (m % 2 + 1) * P],
                            rhs=ident_f32[:], is_transpose=True, start=(term is cell_i), stop=(term is cell_f),
                        )
                nc.scalar.activation(
                    out=row["values"][:, half * ROWS : (half + 1) * ROWS], in_=bank[:], func=ACT.Identity,
                    accum_out=row["sums"][:, half : half + 1],
                )

        def centre(out, row, gain):
            nc.vector.scalar_tensor_tensor(
                out=out[:], in0=row["values"][:], scalar=row["neg_mean"], in1=unit_vectors[gain][:],
                op0=ALU.add, op1=ALU.mult,
            )

        def shift(out, row, vector, units):
            nc.vector.scalar_tensor_tensor(
                out=out[:, units], in0=out[:, units], scalar=row["inv_std"], in1=unit_vectors[vector][:, units],
                op0=ALU.mult, op1=ALU.add,
            )

        def shift_cell(m):
            new_c = cells[m]["new_c"]
            for units in parts(m):
                shift(new_c, cells[m], "shift_c", units)
                nc.sync.dma_start(out=out_1[m * P : (m + 1) * P, units], in_=new_c[:, units])

        def finish_h(m):
            values = cells[m]["values"]
            for units in parts(m):
                nc.vector.tensor_tensor(
                    out=values[:, units], in0=rows[GATES - 1, m]["normed"][:, units], in1=values[:, units], op=ALU.mult,
                )
                nc.sync.dma_start(out=out_0[m * P : (m + 1) * P, units], in_=values[:, units])


        ctx.enter_context(tc.manual_schedule())

        activated = {}
        cell_i = keep.tile([P, UNIT_BLOCKS, 2 * P], F32)
        cell_f = keep.tile([P, UNIT_BLOCKS, 2 * P], F32)
        for i, name in enumerate(("x", "h")):
            load_act(name, 0)
            load_step(PASSES * i)
            load_embedding(name, 0)
            load_small_weight(0, name)
        load_embedding("b", 0)
        load_small_weight(0, "b")
        vector_rows = scratch.tile([P, P], BF16, name="vector_rows", tag="squares")
        nc.vector.memset(vector_rows[:], 0.0)
        for i, vector in enumerate((ln_gamma, ln_beta)):
            nc.sync.dma_start(
                out=vector_rows[i * GATES * UNIT_BLOCKS : (i + 1) * GATES * UNIT_BLOCKS, :],
                in_=vector.rearrange("g (j p) -> (g j) p", p=P),
            )
        first_row = const.tile([P, P], BF16)
        nc.vector.memset(first_row[:], 0.0)
        nc.vector.memset(first_row[0:1, :], 1.0)
        bias_rows = keep.tile([P, GATES * H], BF16)

        def load_bias(position):
            units = slice(GATE_ORDER[position] * H, (GATE_ORDER[position] + 1) * H)
            nc.sync.dma_start(out=bias_rows[:, units], in_=bias[units].partition_broadcast(P))

        load_bias(0)

        waiting = []
        for i, name in enumerate(("x", "h")):
            for g in range(PASSES):
                grouped = turn_act(name, g, g == 1)
                waiting.append((quantise_act, (name, 0, g, grouped)))
                if len(waiting) > 1:
                    function, arguments = waiting.pop(0)
                    function(*arguments)
            for q in range(PASSES * i, PASSES * (i + 1)):
                for pair in range(2):
                    turn_step(q, pair, pair == 1)
                waiting.append((quantise_step, (q,)))
                if len(waiting) > 1:
                    function, arguments = waiting.pop(0)
                    function(*arguments)
            turn_embedding(name, 0)
            turn_small_weight(0, name)
        for function, arguments in waiting:
            function(*arguments)
        turn_embedding("b", 0)
        turn_small_weight(0, "b")

        unit_columns = const.tile([P, P], F32)
        vector_bank = psum_turn.tile([P, P], BF16, tag="turned", name="turned_vectors")
        nc.tensor.transpose(vector_bank[:], vector_rows[:], ident_bf16[:])
        nc.scalar.copy(out=unit_columns[:], in_=vector_bank[:])

        act_waiting = []
        gate_banks = [
            (group, position, k)
            for group in GROUPS for position in range(GATES - 1) for k in range(UNIT_BLOCKS // blocks_per_bank(group))
        ]
        all_rows = [(position, m) for position in range(GATES) for m in range(BATCH_TILES)]
        for t in range(quantise_slot(STEPS_PER_HALF_GATE) - TURN_LEAD - LOAD_LEAD, LAST_SLOT + 1):
            is_tile, z_tile = 0 <= t < N_TILES, 0 <= t + 2 < N_TILES
            turned = [q for q in range(STEPS_PER_HALF_GATE, N_STEPS) if quantise_slot(q) == t + TURN_LEAD]
            quantised = [q for q in range(STEPS_PER_HALF_GATE, N_STEPS) if quantise_slot(q) == t]
            products = [b for b in gate_banks if bank_slot(*b) == t - 1]

            for q in range(STEPS_PER_HALF_GATE, N_STEPS, PASSES):
                if quantise_slot(q) == t + TURN_LEAD + LOAD_LEAD:
                    load_step(q)
            for position in range(1, GATES):
                if t == 4 * position - 6:
                    for name in ("x", "h", "b"):
                        load_small_weight(position, name)
            if t in (2, 6, 10):
                load_bias((t + 2) // 4)
            if t == 11:
                shared = big_rows.tile([P, 4, K], BF16, name="big")
                for i, name in enumerate(("x", "h", "b")):
                    emb_rows[name] = shared[:, i, :].rearrange("p (m g) -> p m g", m=2)
                    load_embedding(name, 2 * P)
            if t == 12:
                shared = big_rows.tile([P, 4, K], BF16, name="big")
                for i, name in enumerate(("x", "h")):
                    act_rows[name] = shared[:, 2 * i : 2 * i + 2, :]
                    load_act(name, 2 * P)
            for m in range(BATCH_TILES):
                if t == norm_slot(GATE_ORDER.index(GATE_F), m):
                    c_rows[m] = c_pool.tile([P, H], BF16, name="c_rows")
                    nc.sync.dma_start(out=c_rows[m][:], in_=c[m * P : (m + 1) * P, :])
            if t == 10:
                for name, vector in (
                    ("gain_o", ln_gamma[GATE_O, :]), ("shift_o", ln_beta[GATE_O, :]), ("gain_c", lnc_gamma), ("shift_c", lnc_beta),
                ):
                    unit_vectors[name] = keep.tile([P, H], BF16, name=name)
                    nc.gpsimd.dma_start(out=unit_vectors[name][:], in_=vector.partition_broadcast(P))

            done_rows = [rows[row] for row in all_rows if row_slot(*row) == t - 1]
            done_rows += [cells[m] for m in range(BATCH_TILES) if t == back_slot(m) + 1]
            due_rows = [rows[row] for row in all_rows if norm_slot(*row) == t]
            due_rows += [cells[m] for m in range(BATCH_TILES) if t == back_slot(m) + CELL_LAG]
            for row in done_rows:
                negate_mean(row)

            if is_tile:
                multiply(t, "x")
            for row in due_rows:
                deviation(row)
            if is_tile:
                multiply(t, "h")
            for row in due_rows:
                invert(row)
            for q in quantised[:1]:
                quantise_step(q)
            if 0 <= t < VECTOR_BIAS_TILES:
                add_bias_on_vector(t)
            for q in quantised[1:]:
                quantise_step(q)
            for name, g, grouped in act_waiting:
                quantise_act(name, 2 * P, g, grouped)
            act_waiting = []

            for b in products:
                gate_product(*b)

            for m in range(BATCH_TILES):
                if t == back_slot(m):
                    cell_back(m)

            matmuls = []
            if z_tile:
                matmuls += [(start_z, (t + 2, "x")), (start_z, (t + 2, "h"))]
            if is_tile:
                matmuls += [(start_offset, (t,))] + ([(add_bias, (t,))] if t >= VECTOR_BIAS_TILES else [])
            if is_tile and sums_on_tensor(t):
                matmuls.append((add_transposed, (t,)))
            mx_passes = [(start_product, (t + 1, name)) for name in ("x", "h")] if 0 <= t + 1 < N_TILES else []
            copies = [(copy_z, (t + 2, name)) for name in ("x", "h")] if z_tile else []
            copies.append((start_stats, (done_rows,)))
            transposes = [(turn_step, (q, pair, False)) for q in turned for pair in range(2)]
            transposes += [(gate_bank, b) for b in gate_banks if bank_slot(*b) == t]
            for position in range(1, GATES):
                if 0 <= t - (4 * position - 5) < 3:
                    transposes.append((turn_small_weight, (position, ("x", "h", "b")[t - (4 * position - 5)])))
            if t in (12, 13):
                transposes += [(turn_embedding, (name, 2 * P)) for name in (("x", "h") if t == 12 else ("b",))]
            while matmuls or copies:
                for function, arguments in matmuls[:1] + transposes[:1] + copies[:1]:
                    function(*arguments)
                matmuls, transposes, copies = matmuls[1:], transposes[1:], copies[1:]
            for function, arguments in mx_passes[:1] + transposes + mx_passes[1:]:
                function(*arguments)
            if t in (13, 14):
                name = ("x", "h")[t - 13]
                act_waiting = [(name, g, turn_act(name, g, False)) for g in range(PASSES)]

            for m in range(BATCH_TILES):
                for units in parts(m):
                    if t == back_slot(m) + CELL_LAG + 1:
                        nc.scalar.activation(out=cells[m]["values"][:, units], in_=cells[m]["new_c"][:, units], func=ACT.Tanh)
                    if t == norm_slot(GATES - 1, m) + 1:
                        values = rows[GATES - 1, m]["normed"][:, units]
                        nc.scalar.activation(out=values, in_=values, func=ACT.Sigmoid)

            if is_tile and not sums_on_tensor(t):
                add_products(t)
            normed = []
            for row in all_rows:
                if t == norm_slot(*row):
                    if GATE_ORDER[row[0]] == GATE_O:
                        rows[row]["normed"] = pre_pool.tile([P, H], F32, name="normed_o", tag="pre")
                        centre(rows[row]["normed"], rows[row], "gain_o")
                        normed += [(shift, (rows[row]["normed"], rows[row], "shift_o", units)) for units in parts(row[1])]
                    else:
                        normalise(rows[row])
            for m in range(BATCH_TILES):
                if t == back_slot(m) + CELL_LAG:
                    cells[m]["new_c"] = big_rows.tile([P, H], F32, name="new_c", tag="big")
                    centre(cells[m]["new_c"], cells[m], "gain_c")
                    normed.append((shift_cell, (m,)))
            if is_tile:
                finish_tile(t)
            for function, arguments in normed:
                function(*arguments)
            for m in range(BATCH_TILES):
                if t == new_h_slot(m):
                    finish_h(m)
